import numpy as np
import ml_dtypes


def mxq(x, axis, fmt="e4m3"):
    dtype, down = {"e4m3": (ml_dtypes.float8_e4m3fn, 7), "e5m2": (ml_dtypes.float8_e5m2, 14)}[fmt]
    v = np.moveaxis(np.asarray(x, np.float32).astype(ml_dtypes.bfloat16).astype(np.float64), axis, -1)
    blocks = v.reshape(v.shape[:-1] + (-1, 32))
    amax = np.abs(blocks).max(-1, keepdims=True)
    byte = np.maximum(np.where(amax > 0, np.frexp(amax)[1] - 1 + 127, 0) - down, 1)
    scale = np.exp2(byte - 127.0)
    codes = (blocks / scale).astype(np.float32).astype(dtype).astype(np.float64)
    return np.moveaxis((codes * scale).reshape(v.shape), -1, axis)


WIDE = False


def mx_kscale(k):
    if not WIDE:
        return np.ones(k)
    levels = np.array([10, -10, 5, -5, 0])
    if k % 512:
        return np.exp2(np.random.permutation(np.resize(levels, k // 32))).repeat(32)
    a = np.empty((k // 512, 16))
    for p in range(k // 512):
        a[p, :8] = np.random.permutation(np.resize(levels, 8))
        for g in range(8):
            far = levels[np.abs(levels - a[p, g]) >= 10]
            a[p, g + 8] = far[np.random.randint(len(far))]
    return np.exp2(a.ravel()).repeat(32)


BF16 = ml_dtypes.bfloat16


def bf(x):
    return np.asarray(x, np.float32).astype(BF16)


def f64(x):
    return np.asarray(x).astype(np.float64)


B, DI, DH, H, DP = 512, 1024, 1024, 4, 1536
HD = DH // H
EPS = 1e-5


def sigmoid(v):
    return 1.0 / (1.0 + np.exp(-v))


def setup_inputs():
    s = mx_kscale(DI)
    d = {"x": bf(np.random.standard_normal((B, DI)) * 1.5 + np.random.standard_normal((B, 1)) * 0.5),
         "h_prev": bf(np.random.standard_normal((B, DH)) * 0.5),
         "c_prev": bf(np.random.standard_normal((B, DH))),
         "n_prev": bf(0.5 + np.abs(np.random.standard_normal((B, DH)))),
         "m_prev": bf(np.random.standard_normal((B, DH))),
         "ln_w": bf((1.0 + 0.1 * np.random.standard_normal(DI)) * s),
         "ln_b": bf(0.2 * np.random.standard_normal(DI) * s)}
    for g in "zifo":
        d["W" + g] = bf(np.random.standard_normal((DI, DH)) / np.sqrt(DI) / s[:, None])
        d["b_" + g] = bf(0.2 * np.random.standard_normal(DH))
        d["R" + g] = bf(np.random.standard_normal((H, HD, HD)) / np.sqrt(HD))
        d["rb_" + g] = bf(0.2 * np.random.standard_normal(DH))
    return d


def reference(x, h_prev, c_prev, n_prev, m_prev, ln_w, ln_b,
              Wz, b_z, Rz, rb_z, Wi, b_i, Ri, rb_i, Wf, b_f, Rf, rb_f, Wo, b_o, Ro, rb_o):
    x = f64(x)
    mu = x.mean(-1, keepdims=True)
    var = x.var(-1, keepdims=True)
    xn = (x - mu) / np.sqrt(var + EPS) * f64(ln_w) + f64(ln_b)
    xq = mxq(xn, 1, "e4m3")
    hr = f64(h_prev).reshape(B, H, HD).transpose(1, 0, 2)

    def gate(W, b, R, rb):
        rec = (hr @ f64(R)).transpose(1, 0, 2).reshape(B, DH)
        return (xq @ mxq(f64(W), 0, "e4m3")) + f64(b) + (rec + f64(rb))

    z_t = gate(Wz, b_z, Rz, rb_z)
    i_t = gate(Wi, b_i, Ri, rb_i)
    f_t = gate(Wf, b_f, Rf, rb_f)
    o_t = gate(Wo, b_o, Ro, rb_o)
    zt = np.tanh(z_t)
    ot = sigmoid(o_t)
    mt = np.maximum(f_t + f64(m_prev), i_t)
    it = np.exp(i_t - mt)
    ft = np.exp(f_t + f64(m_prev) - mt)
    ct = ft * f64(c_prev) + it * zt
    nt = ft * f64(n_prev) + it
    ht = ot * (ct / (nt + 1e-13))
    return (ht, ct, nt, mt)

@@ -1,0 +1,336 @@
+import math
+
+import concourse.mybir as mybir
+from concourse.masks import make_identity
+
+F32 = mybir.dt.float32
+BF16 = mybir.dt.bfloat16
+U32 = mybir.dt.uint32
+U8 = mybir.dt.uint8
+FP8X4 = mybir.dt.float8_e4m3fn_x4
+ALU = mybir.AluOpType
+ACT = mybir.ActivationFunctionType
+
+P = 128
+B, DI, DH, HEADS = 512, 1024, 1024, 4
+HD = DH // HEADS
+ROW_TILES = B // P
+PACK = 4
+K_PASS = P * PACK
+PASSES = DI // K_PASS
+BANK = 512
+HALVES = DH // BANK
+HEADS_PER_BANK = BANK // HD
+K_TILES = DH // P
+K_TILES_PER_HEAD = HD // P
+LN_EPS = 1e-5
+N_EPS = 1e-13
+GATES = ("i", "f", "z", "o")
+RAW_AHEAD = 3
+PIECE = 256
+
+FLOPS = 2 * B * DI * DH * 4 + 2 * B * DH * HD * 4
+
+
+def runs_of_four_out(grouped):
+    return grouped.rearrange("p (c i) t -> p c t i", i=4)
+
+
+def runs_of_four_in(rows):
+    return rows.rearrange("p t (c i) -> p c t i", i=4)
+
+
+def bank_columns(half):
+    return slice(half * BANK, (half + 1) * BANK)
+
+
+def tile_slstmblock_pa_kernel(
+    tc, x, h_prev, c_prev, n_prev, m_prev, ln_w, ln_b,
+    Wz, b_z, Rz, rb_z, Wi, b_i, Ri, rb_i, Wf, b_f, Rf, rb_f, Wo, b_o, Ro, rb_o,
+    out_0, out_1, out_2, out_3,
+):
+    nc = tc.nc
+    weight = {"z": Wz, "i": Wi, "f": Wf, "o": Wo}
+    recurrent = {"z": Rz, "i": Ri, "f": Rf, "o": Ro}
+    biases = {"z": (b_z, rb_z), "i": (b_i, rb_i), "f": (b_f, rb_f), "o": (b_o, rb_o)}
+    h_out, c_out, n_out, m_out = out_0, out_1, out_2, out_3
+
+    def rows_of(dram, t):
+        return dram[t * P : (t + 1) * P, :]
+
+    def by_row_tile(dram):
+        return dram.rearrange("(t p) n -> p t n", p=P)
+
+    with (
+        tc.tile_pool(name="const", bufs=1) as const,
+        tc.tile_pool(name="state", bufs=1) as state,
+        tc.tile_pool(name="w_raw", bufs=RAW_AHEAD) as w_raw,
+        tc.tile_pool(name="w_grouped", bufs=2) as w_grouped,
+        tc.tile_pool(name="w_quant", bufs=2 * PASSES) as w_quant,
+        tc.psum_pool(name="psum_mx", bufs=4) as psum_mx,
+        tc.psum_pool(name="psum_rec", bufs=2) as psum_rec,
+    ):
+        ident_f32 = const.tile([P, P], F32)
+        make_identity(nc, ident_f32[:])
+        ident_bf16 = const.tile([P, P], BF16)
+        make_identity(nc, ident_bf16[:])
+        ones = const.tile([P, P], BF16)
+        nc.vector.memset(ones[:], 1.0)
+        minus_half = const.tile([P, 1], F32)
+        nc.vector.memset(minus_half[:], -0.5)
+
+        pre = {g: state.tile([P, ROW_TILES, DH], F32, name="pre_" + g) for g in GATES}
+        x_codes = state.tile([P, PASSES * B], U32, align_bytes=64)
+        x_scales = state.tile([P, PASSES * B], U8, align_bytes=64)
+        h_t = state.tile([P, K_TILES, B], BF16)
+        r_sb = {}
+        bias_sb = {}
+
+        chunks = [(gate, g) for gate in GATES for g in range(PASSES)]
+        raw_chunk = {}
+        w_codes = {}
+        w_scales = {}
+
+        def start_weight_load(j):
+            gate, g = chunks[j]
+            raw = w_raw.tile([P, PACK, DH], BF16, name="raw")
+            by_pass = weight[gate].rearrange("(g p t) n -> g p t n", t=PACK, p=P)
+            nc.sync.dma_start(out=raw[:], in_=by_pass[g])
+            raw_chunk[j] = raw
+
+        def regroup_and_quantise(rows, codes, scales):
+            grouped = w_grouped.tile([P, DH, PACK], BF16, name="grouped", align_bytes=64)
+            for c0 in range(0, DH, PIECE):
+                nc.any.tensor_copy(
+                    out=runs_of_four_out(grouped[:, c0 : c0 + PIECE, :]),
+                    in_=runs_of_four_in(rows[:, :, c0 : c0 + PIECE]),
+                )
+            for half in range(HALVES):
+                cols = bank_columns(half)
+                nc.vector.quantize_mx(
+                    out=codes[:, cols].bitcast(FP8X4),
+                    scales=scales[:, cols],
+                    in_=grouped[:, cols, :].rearrange("p c t -> p (c t)"),
+                )
+
+        def prepare_weights(gate):
+            for g in range(PASSES):
+                j = chunks.index((gate, g))
+                codes = w_quant.tile([P, DH], U32, name="codes", align_bytes=64)
+                scales = w_quant.tile([P, DH], U8, name="scales", align_bytes=64)
+                regroup_and_quantise(raw_chunk[j][:], codes[:], scales[:])
+                w_codes[(gate, g)] = codes
+                w_scales[(gate, g)] = scales
+                if j + RAW_AHEAD < len(chunks):
+                    start_weight_load(j + RAW_AHEAD)
+
+        def load_recurrent(pool, gate):
+            r_sb[gate] = pool.tile([P, K_TILES, HD], BF16, name="r_" + gate)
+            nc.sync.dma_start(
+                out=r_sb[gate][:], in_=recurrent[gate].rearrange("h (kt p) n -> p (h kt) n", p=P)
+            )
+
+        def recurrent_part(gate, addend, bias_rows=None):
+            for t in range(ROW_TILES):
+                for half in range(HALVES):
+                    rec = psum_rec.tile([P, BANK], F32, name="rec")
+                    for hh in range(HEADS_PER_BANK):
+                        head = half * HEADS_PER_BANK + hh
+                        group = rec[:, hh * HD : (hh + 1) * HD]
+                        if bias_rows is not None:
+                            nc.tensor.matmul(
+                                out=group, lhsT=ones[:], rhs=bias_rows[:, head * HD : (head + 1) * HD],
+                                start=True, stop=False,
+                            )
+                        for kt in range(K_TILES_PER_HEAD):
+                            k_tile = head * K_TILES_PER_HEAD + kt
+                            nc.tensor.matmul(
+                                out=group,
+                                lhsT=h_t[:, k_tile, t * P : (t + 1) * P],
+                                rhs=r_sb[gate][:, k_tile, :],
+                                start=(kt == 0 and bias_rows is None),
+                                stop=(kt == K_TILES_PER_HEAD - 1),
+                            )
+                    cols = bank_columns(half)
+                    nc.vector.tensor_tensor(
+                        out=pre[gate][:, t, cols], in0=rec[:], in1=addend(t, cols), op=ALU.add
+                    )
+
+        def add_input_part(gate):
+            for t in range(ROW_TILES):
+                for half in range(HALVES):
+                    cols = bank_columns(half)
+                    acc = psum_mx.tile([P, BANK], F32, name="acc")
+                    for g in range(PASSES):
+                        rows = slice(g * B + t * P, g * B + (t + 1) * P)
+                        nc.tensor.matmul_mx(
+                            out=acc[:],
+                            lhsT=x_codes[:, rows].bitcast(FP8X4),
+                            lhsT_scale=x_scales[:, rows],
+                            rhs=w_codes[(gate, g)][:, cols].bitcast(FP8X4),
+                            rhs_scale=w_scales[(gate, g)][:, cols],
+                            start=(g == 0),
+                            stop=(g == PASSES - 1),
+                        )
+                    nc.vector.tensor_tensor(
+                        out=pre[gate][:, t, cols], in0=acc[:], in1=pre[gate][:, t, cols], op=ALU.add
+                    )
+
+        with (
+            tc.tile_pool(name="early", bufs=1) as early,
+            tc.psum_pool(name="psum_tp", bufs=2) as psum_tp,
+        ):
+            x_sb = early.tile([P, ROW_TILES, DI], BF16)
+            for t in range(ROW_TILES):
+                nc.sync.dma_start(out=x_sb[:, t, :], in_=rows_of(x, t))
+            ln_w_raw = early.tile([P, PASSES, PACK], BF16)
+            ln_b_raw = early.tile([P, PASSES, PACK], BF16)
+            nc.scalar.dma_start(out=ln_w_raw[:], in_=ln_w.rearrange("(g p t) -> p g t", p=P, t=PACK))
+            nc.scalar.dma_start(out=ln_b_raw[:], in_=ln_b.rearrange("(g p t) -> p g t", p=P, t=PACK))
+            bias_rows = early.tile([P, len(GATES), DH], BF16)
+            nc.vector.memset(bias_rows[:], 0.0)
+            for gi, gate in enumerate(GATES):
+                for r, vec in enumerate(biases[gate]):
+                    nc.scalar.dma_start(
+                        out=bias_rows[r : r + 1, gi, :], in_=vec.rearrange("(o n) -> o n", o=1)
+                    )
+            h_sb = early.tile([P, ROW_TILES, DH], BF16)
+            for t in range(ROW_TILES):
+                nc.sync.dma_start(out=h_sb[:, t, :], in_=rows_of(h_prev, t))
+            load_recurrent(early, "i")
+            start_weight_load(0)
+            start_weight_load(1)
+            m_sb = early.tile([P, ROW_TILES, DH], BF16)
+            nc.sync.dma_start(out=m_sb[:], in_=by_row_tile(m_prev))
+            load_recurrent(early, "f")
+            start_weight_load(2)
+            load_recurrent(state, "z")
+            load_recurrent(state, "o")
+
+            stats = early.tile([P, ROW_TILES, 2, 6], F32)
+            mean_var = early.tile([P, ROW_TILES, 2], F32)
+            minus_mean = early.tile([P, ROW_TILES], F32)
+            var_eps = early.tile([P, ROW_TILES], F32)
+            rstd = early.tile([P, ROW_TILES], F32)
+            shift = early.tile([P, ROW_TILES], F32)
+            y = early.tile([P, ROW_TILES, DI], F32)
+            for t in range(ROW_TILES):
+                one = slice(t, t + 1)
+                for s in range(2):
+                    nc.vector.bn_stats(out=stats[:, t, s, :], in_=x_sb[:, t, s * 512 : (s + 1) * 512])
+                nc.vector.bn_aggr(out=mean_var[:, t, :], in_=stats[:, t, :, :].rearrange("p s f -> p (s f)"))
+                nc.vector.tensor_scalar(
+                    out=minus_mean[:, one], in0=mean_var[:, t, 0:1], scalar1=-1.0, scalar2=None, op0=ALU.mult
+                )
+                nc.gpsimd.tensor_scalar(
+                    out=var_eps[:, one], in0=mean_var[:, t, 1:2], scalar1=LN_EPS, scalar2=None, op0=ALU.add
+                )
+                nc.gpsimd.tensor_tensor(out=rstd[:, one], in0=var_eps[:, one], in1=minus_half[:], op=ALU.pow)
+                nc.gpsimd.tensor_tensor(out=shift[:, one], in0=minus_mean[:, one], in1=rstd[:, one], op=ALU.mult)
+                nc.scalar.activation(
+                    out=y[:, t, :].rearrange("b (g j p) -> b g j p", j=PACK, p=P),
+                    in_=x_sb[:, t, :].rearrange("b (g p j) -> b g j p", j=PACK, p=P),
+                    func=ACT.Identity, bias=shift[:, one], scale=rstd[:, one],
+                )
+
+            ln_cols = early.tile([P, 16], F32)
+            nc.vector.tensor_copy(out=ln_cols[:, 0:8], in_=ln_w_raw[:].rearrange("p g t -> p (g t)"))
+            nc.vector.tensor_copy(out=ln_cols[:, 8:16], in_=ln_b_raw[:].rearrange("p g t -> p (g t)"))
+
+            for t in range(ROW_TILES):
+                h_ps = psum_tp.tile([P, K_TILES, P], BF16, name="h_ps", tag="tp")
+                for kt in range(K_TILES):
+                    nc.tensor.transpose(h_ps[:, kt, :], h_sb[:, t, kt * P : (kt + 1) * P], ident_bf16[:])
+                nc.any.tensor_copy(out=h_t[:, :, t * P : (t + 1) * P], in_=h_ps[:])
+
+            for gate, pool in (("i", early), ("z", state), ("o", state)):
+                bias_sb[gate] = pool.tile([P, DH], F32, name="bias_" + gate)
+                for half in range(HALVES):
+                    cols = bank_columns(half)
+                    bias_ps = psum_rec.tile([P, BANK], F32, name="bias_ps", tag="rec")
+                    nc.tensor.matmul(
+                        out=bias_ps[:], lhsT=ones[:], rhs=bias_rows[:, GATES.index(gate), cols], start=True, stop=True
+                    )
+                    nc.any.tensor_copy(out=bias_sb[gate][:, cols], in_=bias_ps[:])
+
+            recurrent_part("i", lambda t, cols: bias_sb["i"][:, cols])
+            prepare_weights("i")
+
+            xn_t = early.tile([P, PACK, PASSES * B], BF16)
+            for g in range(PASSES):
+                for t4 in range(PACK):
+                    r = g * PACK + t4
+                    y_ps = psum_tp.tile([P, B], F32, name="y_ps", tag="tp")
+                    for t in range(ROW_TILES):
+                        nc.tensor.transpose(y_ps[:, t * P : (t + 1) * P], y[:, t, r * P : (r + 1) * P], ident_f32[:])
+                    nc.scalar.activation(
+                        out=xn_t[:, t4, g * B : (g + 1) * B], in_=y_ps[:], func=ACT.Identity,
+                        bias=ln_cols[:, 8 + r : 9 + r], scale=ln_cols[:, r : r + 1],
+                    )
+            regroup_and_quantise(xn_t[:], x_codes[:], x_scales[:])
+
+            recurrent_part("f", lambda t, cols: m_sb[:, t, cols], bias_rows=bias_rows[:, GATES.index("f"), :])
+            prepare_weights("f")
+
+        with tc.tile_pool(name="late", bufs=1) as late:
+            n_sb = late.tile([P, ROW_TILES, DH], BF16)
+            nc.sync.dma_start(out=n_sb[:], in_=by_row_tile(n_prev))
+            c_sb = late.tile([P, ROW_TILES, DH], BF16)
+            nc.sync.dma_start(out=c_sb[:], in_=by_row_tile(c_prev))
+            m_new = late.tile([P, ROW_TILES, DH], F32)
+            n_new = late.tile([P, ROW_TILES, DH], F32)
+            recip = late.tile([P, ROW_TILES, DH], F32)
+
+            add_input_part("i")
+            for t in range(ROW_TILES):
+                nc.gpsimd.tensor_tensor(out=pre["f"][:, t, :], in0=pre["f"][:, t, :], in1=pre["i"][:, t, :], op=ALU.subtract)
+            add_input_part("f")
+            for t in range(ROW_TILES):
+                big_i, d = pre["i"][:, t, :], pre["f"][:, t, :]
+                nc.vector.scalar_tensor_tensor(
+                    out=m_new[:, t, :], in0=d, scalar=0.0, in1=big_i, op0=ALU.max, op1=ALU.add
+                )
+                nc.sync.dma_start(out=rows_of(m_out, t), in_=m_new[:, t, :])
+                nc.scalar.activation(out=big_i, in_=d, func=ACT.Exp, scale=-1.0)
+                nc.scalar.activation(out=d, in_=d, func=ACT.Exp)
+            for t in range(ROW_TILES):
+                exp_minus_d, exp_d = pre["i"][:, t, :], pre["f"][:, t, :]
+                nc.vector.scalar_tensor_tensor(
+                    out=n_new[:, t, :], in0=exp_d, scalar=1.0, in1=n_sb[:, t, :], op0=ALU.min, op1=ALU.mult
+                )
+                nc.vector.scalar_tensor_tensor(
+                    out=n_new[:, t, :], in0=exp_minus_d, scalar=1.0, in1=n_new[:, t, :], op0=ALU.min, op1=ALU.add
+                )
+                nc.sync.dma_start(out=rows_of(n_out, t), in_=n_new[:, t, :])
+                nc.vector.scalar_tensor_tensor(
+                    out=exp_d, in0=exp_d, scalar=1.0, in1=c_sb[:, t, :], op0=ALU.min, op1=ALU.mult
+                )
+            nc.scalar.activation(out=recip[:], in_=n_new[:], func=ACT.Ln, bias=N_EPS)
+            for t in range(ROW_TILES):
+                nc.scalar.activation(
+                    out=recip[:, t, :], in_=recip[:, t, :], func=ACT.Exp, bias=math.log(0.5), scale=-1.0
+                )
+
+            recurrent_part("z", lambda t, cols: bias_sb["z"][:, cols])
+            prepare_weights("z")
+            add_input_part("z")
+            for t in range(ROW_TILES):
+                exp_minus_d, f_c, z = pre["i"][:, t, :], pre["f"][:, t, :], pre["z"][:, t, :]
+                nc.scalar.activation(out=z, in_=z, func=ACT.Tanh)
+                nc.vector.scalar_tensor_tensor(
+                    out=z, in0=exp_minus_d, scalar=1.0, in1=z, op0=ALU.min, op1=ALU.mult
+                )
+                nc.gpsimd.tensor_tensor(out=f_c, in0=f_c, in1=z, op=ALU.add)
+                nc.sync.dma_start(out=rows_of(c_out, t), in_=f_c)
+                nc.gpsimd.tensor_tensor(out=recip[:, t, :], in0=recip[:, t, :], in1=f_c, op=ALU.mult)
+
+            recurrent_part("o", lambda t, cols: bias_sb["o"][:, cols])
+            prepare_weights("o")
+            add_input_part("o")
+            for t in range(ROW_TILES):
+                o = pre["o"][:, t, :]
+                nc.scalar.activation(out=o, in_=o, func=ACT.Tanh, scale=0.5)
+                nc.vector.scalar_tensor_tensor(
+                    out=o, in0=o, scalar=1.0, in1=recip[:, t, :], op0=ALU.add, op1=ALU.mult
+                )
+                nc.sync.dma_start(out=rows_of(h_out, t), in_=o)

@@ -27,7 +27,6 @@ LN_EPS = 1e-5
 N_EPS = 1e-13
 GATES = ("i", "f", "z", "o")
 RAW_AHEAD = 3
-PIECE = 256
 
 FLOPS = 2 * B * DI * DH * 4 + 2 * B * DH * HD * 4
 
@@ -62,32 +61,27 @@ def tile_slstmblock_pa_kernel(
         return dram.rearrange("(t p) n -> p t n", p=P)
 
     with (
+        tc.manual_schedule(),
         tc.tile_pool(name="const", bufs=1) as const,
         tc.tile_pool(name="state", bufs=1) as state,
         tc.tile_pool(name="w_raw", bufs=RAW_AHEAD) as w_raw,
-        tc.tile_pool(name="w_grouped", bufs=2) as w_grouped,
-        tc.tile_pool(name="w_quant", bufs=2 * PASSES) as w_quant,
-        tc.psum_pool(name="psum_mx", bufs=4) as psum_mx,
-        tc.psum_pool(name="psum_rec", bufs=2) as psum_rec,
+        tc.tile_pool(name="w_grouped", bufs=3) as w_grouped,
+        tc.tile_pool(name="w_quant", bufs=len(GATES) * PASSES) as w_quant,
+        tc.psum_pool(name="psum", bufs=8) as psum,
     ):
-        ident_f32 = const.tile([P, P], F32)
-        make_identity(nc, ident_f32[:])
-        ident_bf16 = const.tile([P, P], BF16)
-        make_identity(nc, ident_bf16[:])
-        ones = const.tile([P, P], BF16)
-        nc.vector.memset(ones[:], 1.0)
-        minus_half = const.tile([P, 1], F32)
-        nc.vector.memset(minus_half[:], -0.5)
-
-        pre = {g: state.tile([P, ROW_TILES, DH], F32, name="pre_" + g) for g in GATES}
+        pre_i = state.tile([P, ROW_TILES, DH], F32)
+        pre_f = state.tile([P, ROW_TILES, DH], F32)
         x_codes = state.tile([P, PASSES * B], U32, align_bytes=64)
         x_scales = state.tile([P, PASSES * B], U8, align_bytes=64)
         h_t = state.tile([P, K_TILES, B], BF16)
+        m_sb = state.tile([P, ROW_TILES, DH], BF16)
+        bias_rows = state.tile([P, DH], BF16)
         r_sb = {}
         bias_sb = {}
 
         chunks = [(gate, g) for gate in GATES for g in range(PASSES)]
         raw_chunk = {}
+        grouped_chunk = {}
         w_codes = {}
         w_scales = {}
 
@@ -98,31 +92,32 @@ def tile_slstmblock_pa_kernel(
             nc.sync.dma_start(out=raw[:], in_=by_pass[g])
             raw_chunk[j] = raw
 
-        def regroup_and_quantise(rows, codes, scales):
-            grouped = w_grouped.tile([P, DH, PACK], BF16, name="grouped", align_bytes=64)
-            for c0 in range(0, DH, PIECE):
-                nc.any.tensor_copy(
-                    out=runs_of_four_out(grouped[:, c0 : c0 + PIECE, :]),
-                    in_=runs_of_four_in(rows[:, :, c0 : c0 + PIECE]),
-                )
-            for half in range(HALVES):
-                cols = bank_columns(half)
-                nc.vector.quantize_mx(
-                    out=codes[:, cols].bitcast(FP8X4),
-                    scales=scales[:, cols],
-                    in_=grouped[:, cols, :].rearrange("p c t -> p (c t)"),
-                )
+        def regroup(rows, grouped, half, copy):
+            cols = bank_columns(half)
+            copy(out=runs_of_four_out(grouped[:, cols, :]), in_=runs_of_four_in(rows[:, :, cols]))
 
-        def prepare_weights(gate):
-            for g in range(PASSES):
-                j = chunks.index((gate, g))
-                codes = w_quant.tile([P, DH], U32, name="codes", align_bytes=64)
-                scales = w_quant.tile([P, DH], U8, name="scales", align_bytes=64)
-                regroup_and_quantise(raw_chunk[j][:], codes[:], scales[:])
-                w_codes[(gate, g)] = codes
-                w_scales[(gate, g)] = scales
-                if j + RAW_AHEAD < len(chunks):
-                    start_weight_load(j + RAW_AHEAD)
+        def quantise(grouped, codes, scales, half):
+            cols = bank_columns(half)
+            nc.vector.quantize_mx(
+                out=codes[:, cols].bitcast(FP8X4),
+                scales=scales[:, cols],
+                in_=grouped[:, cols, :].rearrange("p c t -> p (c t)"),
+            )
+
+        def regroup_weight(j, half, copy):
+            if half == 0:
+                grouped_chunk[j] = w_grouped.tile([P, DH, PACK], BF16, name="grouped", align_bytes=64)
+            regroup(raw_chunk[j], grouped_chunk[j], half, copy)
+            if half == HALVES - 1 and j + RAW_AHEAD < len(chunks):
+                start_weight_load(j + RAW_AHEAD)
+
+        def quantise_weight(j):
+            codes = w_quant.tile([P, DH], U32, name="codes", align_bytes=64)
+            scales = w_quant.tile([P, DH], U8, name="scales", align_bytes=64)
+            for half in range(HALVES):
+                quantise(grouped_chunk[j], codes, scales, half)
+            w_codes[chunks[j]] = codes
+            w_scales[chunks[j]] = scales
 
         def load_recurrent(pool, gate):
             r_sb[gate] = pool.tile([P, K_TILES, HD], BF16, name="r_" + gate)
@@ -130,56 +125,58 @@ def tile_slstmblock_pa_kernel(
                 out=r_sb[gate][:], in_=recurrent[gate].rearrange("h (kt p) n -> p (h kt) n", p=P)
             )
 
-        def recurrent_part(gate, addend, bias_rows=None):
-            for t in range(ROW_TILES):
-                for half in range(HALVES):
-                    rec = psum_rec.tile([P, BANK], F32, name="rec")
-                    for hh in range(HEADS_PER_BANK):
-                        head = half * HEADS_PER_BANK + hh
-                        group = rec[:, hh * HD : (hh + 1) * HD]
-                        if bias_rows is not None:
-                            nc.tensor.matmul(
-                                out=group, lhsT=ones[:], rhs=bias_rows[:, head * HD : (head + 1) * HD],
-                                start=True, stop=False,
-                            )
-                        for kt in range(K_TILES_PER_HEAD):
-                            k_tile = head * K_TILES_PER_HEAD + kt
-                            nc.tensor.matmul(
-                                out=group,
-                                lhsT=h_t[:, k_tile, t * P : (t + 1) * P],
-                                rhs=r_sb[gate][:, k_tile, :],
-                                start=(kt == 0 and bias_rows is None),
-                                stop=(kt == K_TILES_PER_HEAD - 1),
-                            )
-                    cols = bank_columns(half)
-                    nc.vector.tensor_tensor(
-                        out=pre[gate][:, t, cols], in0=rec[:], in1=addend(t, cols), op=ALU.add
-                    )
+        def bank(name):
+            return psum.tile([P, BANK], F32, name=name, tag="bank")
 
-        def add_input_part(gate):
-            for t in range(ROW_TILES):
-                for half in range(HALVES):
-                    cols = bank_columns(half)
-                    acc = psum_mx.tile([P, BANK], F32, name="acc")
-                    for g in range(PASSES):
-                        rows = slice(g * B + t * P, g * B + (t + 1) * P)
-                        nc.tensor.matmul_mx(
-                            out=acc[:],
-                            lhsT=x_codes[:, rows].bitcast(FP8X4),
-                            lhsT_scale=x_scales[:, rows],
-                            rhs=w_codes[(gate, g)][:, cols].bitcast(FP8X4),
-                            rhs_scale=w_scales[(gate, g)][:, cols],
-                            start=(g == 0),
-                            stop=(g == PASSES - 1),
-                        )
-                    nc.vector.tensor_tensor(
-                        out=pre[gate][:, t, cols], in0=acc[:], in1=pre[gate][:, t, cols], op=ALU.add
+        def recurrent_bank(gate, t, half, with_m_and_bias=False):
+            rec = bank("rec")
+            for hh in range(HEADS_PER_BANK):
+                head = half * HEADS_PER_BANK + hh
+                group = rec[:, hh * HD : (hh + 1) * HD]
+                cols = slice(head * HD, (head + 1) * HD)
+                if with_m_and_bias:
+                    nc.tensor.matmul(out=group, lhsT=ident_bf16[:], rhs=m_sb[:, t, cols], start=True, stop=False)
+                    nc.tensor.matmul(out=group, lhsT=ones[:], rhs=bias_rows[:, cols], start=False, stop=False)
+                for kt in range(K_TILES_PER_HEAD):
+                    k_tile = head * K_TILES_PER_HEAD + kt
+                    nc.tensor.matmul(
+                        out=group,
+                        lhsT=h_t[:, k_tile, t * P : (t + 1) * P],
+                        rhs=r_sb[gate][:, k_tile, :],
+                        start=(kt == 0 and not with_m_and_bias),
+                        stop=(kt == K_TILES_PER_HEAD - 1),
                     )
+            return rec
 
-        with (
-            tc.tile_pool(name="early", bufs=1) as early,
-            tc.psum_pool(name="psum_tp", bufs=2) as psum_tp,
-        ):
+        def input_bank(gate, t, half):
+            cols = bank_columns(half)
+            acc = bank("acc")
+            for g in range(PASSES):
+                rows = slice(g * B + t * P, g * B + (t + 1) * P)
+                nc.tensor.matmul_mx(
+                    out=acc[:],
+                    lhsT=x_codes[:, rows].bitcast(FP8X4),
+                    lhsT_scale=x_scales[:, rows],
+                    rhs=w_codes[(gate, g)][:, cols].bitcast(FP8X4),
+                    rhs_scale=w_scales[(gate, g)][:, cols],
+                    start=(g == 0),
+                    stop=(g == PASSES - 1),
+                )
+            return acc
+
+        def biased_recurrent(gate, t, out):
+            for half in range(HALVES):
+                cols = bank_columns(half)
+                rec = recurrent_bank(gate, t, half)
+                nc.vector.tensor_tensor(out=out[:, cols], in0=rec[:], in1=bias_sb[gate][:, cols], op=ALU.add)
+
+        def add_input(gate, t, out):
+            for half in range(HALVES):
+                cols = bank_columns(half)
+                acc = input_bank(gate, t, half)
+                nc.vector.tensor_tensor(out=out[:, cols], in0=acc[:], in1=out[:, cols], op=ALU.add)
+
+        with tc.tile_pool(name="early", bufs=1) as early:
             x_sb = early.tile([P, ROW_TILES, DI], BF16)
             for t in range(ROW_TILES):
                 nc.sync.dma_start(out=x_sb[:, t, :], in_=rows_of(x, t))
@@ -187,25 +184,36 @@ def tile_slstmblock_pa_kernel(
             ln_b_raw = early.tile([P, PASSES, PACK], BF16)
             nc.scalar.dma_start(out=ln_w_raw[:], in_=ln_w.rearrange("(g p t) -> p g t", p=P, t=PACK))
             nc.scalar.dma_start(out=ln_b_raw[:], in_=ln_b.rearrange("(g p t) -> p g t", p=P, t=PACK))
-            bias_rows = early.tile([P, len(GATES), DH], BF16)
-            nc.vector.memset(bias_rows[:], 0.0)
-            for gi, gate in enumerate(GATES):
-                for r, vec in enumerate(biases[gate]):
-                    nc.scalar.dma_start(
-                        out=bias_rows[r : r + 1, gi, :], in_=vec.rearrange("(o n) -> o n", o=1)
+            minus_half = const.tile([P, 1], F32)
+            nc.gpsimd.memset(minus_half[:], -0.5)
+            vec_rows = {}
+
+            def load_bias_rows(name, gates):
+                rows = early.tile([P, P], BF16, name="vec_rows_" + name)
+                nc.gpsimd.memset(rows[:], 0.0)
+                vecs = [biases[gate][0] for gate in gates] + [biases[gate][1] for gate in gates]
+                for v, vec in enumerate(vecs):
+                    nc.gpsimd.dma_start(
+                        out=rows[v * K_TILES : (v + 1) * K_TILES, :], in_=vec.rearrange("(r c) -> r c", c=P)
                     )
-            h_sb = early.tile([P, ROW_TILES, DH], BF16)
-            for t in range(ROW_TILES):
-                nc.sync.dma_start(out=h_sb[:, t, :], in_=rows_of(h_prev, t))
-            load_recurrent(early, "i")
+                vec_rows[name] = rows
+
+            load_bias_rows("i", ("i",))
             start_weight_load(0)
+            h_sb = early.tile([P, ROW_TILES, DH], BF16)
+            nc.sync.dma_start(out=h_sb[:], in_=by_row_tile(h_prev))
             start_weight_load(1)
-            m_sb = early.tile([P, ROW_TILES, DH], BF16)
-            nc.sync.dma_start(out=m_sb[:], in_=by_row_tile(m_prev))
-            load_recurrent(early, "f")
+            load_recurrent(early, "i")
             start_weight_load(2)
+            load_recurrent(state, "f")
+            nc.sync.dma_start(out=m_sb[:], in_=by_row_tile(m_prev))
             load_recurrent(state, "z")
             load_recurrent(state, "o")
+
+            warm = const.tile([P, 1], F32)
+            nc.scalar.activation(out=warm[:], in_=minus_half[:], func=ACT.Exp)
+            ident_f32 = const.tile([P, P], F32)
+            make_identity(nc, ident_f32[:])
 
             stats = early.tile([P, ROW_TILES, 2, 6], F32)
             mean_var = early.tile([P, ROW_TILES, 2], F32)
@@ -219,118 +227,207 @@ def tile_slstmblock_pa_kernel(
                 for s in range(2):
                     nc.vector.bn_stats(out=stats[:, t, s, :], in_=x_sb[:, t, s * 512 : (s + 1) * 512])
                 nc.vector.bn_aggr(out=mean_var[:, t, :], in_=stats[:, t, :, :].rearrange("p s f -> p (s f)"))
-                nc.vector.tensor_scalar(
-                    out=minus_mean[:, one], in0=mean_var[:, t, 0:1], scalar1=-1.0, scalar2=None, op0=ALU.mult
-                )
                 nc.gpsimd.tensor_scalar(
                     out=var_eps[:, one], in0=mean_var[:, t, 1:2], scalar1=LN_EPS, scalar2=None, op0=ALU.add
                 )
                 nc.gpsimd.tensor_tensor(out=rstd[:, one], in0=var_eps[:, one], in1=minus_half[:], op=ALU.pow)
+                nc.gpsimd.tensor_scalar(
+                    out=minus_mean[:, one], in0=mean_var[:, t, 0:1], scalar1=-1.0, scalar2=None, op0=ALU.mult
+                )
                 nc.gpsimd.tensor_tensor(out=shift[:, one], in0=minus_mean[:, one], in1=rstd[:, one], op=ALU.mult)
                 nc.scalar.activation(
                     out=y[:, t, :].rearrange("b (g j p) -> b g j p", j=PACK, p=P),
                     in_=x_sb[:, t, :].rearrange("b (g p j) -> b g j p", j=PACK, p=P),
                     func=ACT.Identity, bias=shift[:, one], scale=rstd[:, one],
                 )
-
-            ln_cols = early.tile([P, 16], F32)
+            ln_cols = early.tile([P, 2 * PASSES * PACK], F32)
             nc.vector.tensor_copy(out=ln_cols[:, 0:8], in_=ln_w_raw[:].rearrange("p g t -> p (g t)"))
             nc.vector.tensor_copy(out=ln_cols[:, 8:16], in_=ln_b_raw[:].rearrange("p g t -> p (g t)"))
 
-            for t in range(ROW_TILES):
-                h_ps = psum_tp.tile([P, K_TILES, P], BF16, name="h_ps", tag="tp")
-                for kt in range(K_TILES):
-                    nc.tensor.transpose(h_ps[:, kt, :], h_sb[:, t, kt * P : (kt + 1) * P], ident_bf16[:])
-                nc.any.tensor_copy(out=h_t[:, :, t * P : (t + 1) * P], in_=h_ps[:])
+            ident_bf16 = const.tile([P, P], BF16)
+            make_identity(nc, ident_bf16[:])
+            ones = const.tile([P, P], BF16)
+            nc.gpsimd.memset(ones[:], 1.0)
+            load_bias_rows("zo", ("z", "o"))
+            nc.gpsimd.memset(bias_rows[:], 0.0)
+            for r, vec in enumerate(biases["f"]):
+                nc.gpsimd.dma_start(out=bias_rows[r : r + 1, :], in_=vec.rearrange("(o n) -> o n", o=1))
 
-            for gate, pool in (("i", early), ("z", state), ("o", state)):
-                bias_sb[gate] = pool.tile([P, DH], F32, name="bias_" + gate)
+            def bias_columns(name, n_gates):
+                vec_ps = psum.tile([P, P], BF16, name="vec_ps", tag="bank")
+                nc.tensor.transpose(vec_ps[:], vec_rows[name][:], ident_bf16[:])
+                n_cols = n_gates * K_TILES
+                rb_cols = const.tile([P, n_cols], F32, name="rb_cols_" + name)
+                b_cols = const.tile([P, n_cols], F32, name="b_cols_" + name)
+                nc.vector.tensor_copy(out=rb_cols[:], in_=vec_ps[:, n_cols : 2 * n_cols])
+                nc.vector.tensor_tensor(out=b_cols[:], in0=vec_ps[:, 0:n_cols], in1=rb_cols[:], op=ALU.add)
+                return b_cols
+
+            def spread_bias(gate, b_cols, first):
+                bias_sb[gate] = state.tile([P, DH], F32, name="bias_" + gate)
                 for half in range(HALVES):
-                    cols = bank_columns(half)
-                    bias_ps = psum_rec.tile([P, BANK], F32, name="bias_ps", tag="rec")
-                    nc.tensor.matmul(
-                        out=bias_ps[:], lhsT=ones[:], rhs=bias_rows[:, GATES.index(gate), cols], start=True, stop=True
-                    )
-                    nc.any.tensor_copy(out=bias_sb[gate][:, cols], in_=bias_ps[:])
+                    bias_ps = bank("bias_ps")
+                    for q in range(BANK // P):
+                        c = first + half * (BANK // P) + q
+                        nc.tensor.transpose(
+                            bias_ps[:, q * P : (q + 1) * P], b_cols[:, c : c + 1].to_broadcast([P, P]), ident_f32[:]
+                        )
+                    nc.scalar.copy(out=bias_sb[gate][:, bank_columns(half)], in_=bias_ps[:])
 
-            recurrent_part("i", lambda t, cols: bias_sb["i"][:, cols])
-            prepare_weights("i")
+            for half in range(HALVES):
+                regroup_weight(0, half, nc.vector.tensor_copy)
+            quantise_weight(0)
 
             xn_t = early.tile([P, PACK, PASSES * B], BF16)
+            x_grouped = w_grouped.tile([P, PASSES * B, PACK], BF16, name="grouped", align_bytes=64)
             for g in range(PASSES):
                 for t4 in range(PACK):
                     r = g * PACK + t4
-                    y_ps = psum_tp.tile([P, B], F32, name="y_ps", tag="tp")
+                    y_ps = bank("y_ps")
                     for t in range(ROW_TILES):
                         nc.tensor.transpose(y_ps[:, t * P : (t + 1) * P], y[:, t, r * P : (r + 1) * P], ident_f32[:])
                     nc.scalar.activation(
                         out=xn_t[:, t4, g * B : (g + 1) * B], in_=y_ps[:], func=ACT.Identity,
                         bias=ln_cols[:, 8 + r : 9 + r], scale=ln_cols[:, r : r + 1],
                     )
-            regroup_and_quantise(xn_t[:], x_codes[:], x_scales[:])
+                if g == 0:
+                    i_cols = bias_columns("i", 1)
+                regroup(xn_t, x_grouped, g, nc.vector.tensor_copy)
+            for g in range(PASSES):
+                quantise(x_grouped, x_codes, x_scales, g)
+            spread_bias("i", i_cols, 0)
 
-            recurrent_part("f", lambda t, cols: m_sb[:, t, cols], bias_rows=bias_rows[:, GATES.index("f"), :])
-            prepare_weights("f")
+            for t in range(ROW_TILES):
+                h_ps = psum.tile([P, K_TILES, P], BF16, name="h_ps", tag="bank")
+                for kt in range(K_TILES):
+                    nc.tensor.transpose(h_ps[:, kt, :], h_sb[:, t, kt * P : (kt + 1) * P], ident_bf16[:])
+                nc.scalar.copy(out=h_t[:, :, t * P : (t + 1) * P], in_=h_ps[:])
 
-        with tc.tile_pool(name="late", bufs=1) as late:
+            for half in range(HALVES):
+                regroup_weight(1, half, nc.scalar.copy)
+            for t in range(ROW_TILES):
+                biased_recurrent("i", t, pre_i[:, t, :])
+            zo_cols = bias_columns("zo", 2)
+            quantise_weight(1)
+
+        with (
+            tc.tile_pool(name="late", bufs=1) as late,
+            tc.tile_pool(name="stream", bufs=5) as stream,
+        ):
             n_sb = late.tile([P, ROW_TILES, DH], BF16)
-            nc.sync.dma_start(out=n_sb[:], in_=by_row_tile(n_prev))
             c_sb = late.tile([P, ROW_TILES, DH], BF16)
-            nc.sync.dma_start(out=c_sb[:], in_=by_row_tile(c_prev))
-            m_new = late.tile([P, ROW_TILES, DH], F32)
             n_new = late.tile([P, ROW_TILES, DH], F32)
             recip = late.tile([P, ROW_TILES, DH], F32)
 
-            add_input_part("i")
+            spread_bias("z", zo_cols, 0)
+            spread_bias("o", zo_cols, K_TILES)
+            for half in range(HALVES):
+                regroup_weight(2, half, nc.scalar.copy)
+            nc.sync.dma_start(out=n_sb[:], in_=by_row_tile(n_prev))
+            nc.sync.dma_start(out=c_sb[:], in_=by_row_tile(c_prev))
+            for half in range(HALVES):
+                regroup_weight(3, half, nc.scalar.copy)
+            for half in range(HALVES):
+                regroup_weight(4, half, nc.scalar.copy)
+
+            def forget_banks(t):
+                return [recurrent_bank("f", t, half, with_m_and_bias=True) for half in range(HALVES)]
+
+            def forget_less_input(t, recs):
+                for half, rec in enumerate(recs):
+                    cols = bank_columns(half)
+                    nc.vector.tensor_tensor(
+                        out=pre_f[:, t, cols], in0=rec[:], in1=pre_i[:, t, cols], op=ALU.subtract
+                    )
+
+            recs = {}
             for t in range(ROW_TILES):
-                nc.gpsimd.tensor_tensor(out=pre["f"][:, t, :], in0=pre["f"][:, t, :], in1=pre["i"][:, t, :], op=ALU.subtract)
-            add_input_part("f")
-            for t in range(ROW_TILES):
-                big_i, d = pre["i"][:, t, :], pre["f"][:, t, :]
-                nc.vector.scalar_tensor_tensor(
-                    out=m_new[:, t, :], in0=d, scalar=0.0, in1=big_i, op0=ALU.max, op1=ALU.add
-                )
-                nc.sync.dma_start(out=rows_of(m_out, t), in_=m_new[:, t, :])
-                nc.scalar.activation(out=big_i, in_=d, func=ACT.Exp, scale=-1.0)
-                nc.scalar.activation(out=d, in_=d, func=ACT.Exp)
-            for t in range(ROW_TILES):
-                exp_minus_d, exp_d = pre["i"][:, t, :], pre["f"][:, t, :]
+                add_input("i", t, pre_i[:, t, :])
+                recs[t] = forget_banks(t)
+                if t > 0:
+                    forget_less_input(t - 1, recs[t - 1])
+                if t == 1:
+                    quantise_weight(2)
+            forget_less_input(ROW_TILES - 1, recs[ROW_TILES - 1])
+            quantise_weight(3)
+
+            def n_and_forget(t):
+                exp_minus_d, exp_d = pre_i[:, t, :], pre_f[:, t, :]
                 nc.vector.scalar_tensor_tensor(
                     out=n_new[:, t, :], in0=exp_d, scalar=1.0, in1=n_sb[:, t, :], op0=ALU.min, op1=ALU.mult
+                )
+                nc.vector.scalar_tensor_tensor(
+                    out=exp_d, in0=exp_d, scalar=1.0, in1=c_sb[:, t, :], op0=ALU.min, op1=ALU.mult
                 )
                 nc.vector.scalar_tensor_tensor(
                     out=n_new[:, t, :], in0=exp_minus_d, scalar=1.0, in1=n_new[:, t, :], op0=ALU.min, op1=ALU.add
                 )
                 nc.sync.dma_start(out=rows_of(n_out, t), in_=n_new[:, t, :])
-                nc.vector.scalar_tensor_tensor(
-                    out=exp_d, in0=exp_d, scalar=1.0, in1=c_sb[:, t, :], op0=ALU.min, op1=ALU.mult
-                )
-            nc.scalar.activation(out=recip[:], in_=n_new[:], func=ACT.Ln, bias=N_EPS)
+
+            def gate_tile(name):
+                return stream.tile([P, DH], F32, name=name, tag="wide")
+
+            z = {}
+            o = {}
+
+            def pre_tanh(gate, tiles, t, scale):
+                add_input(gate, t, tiles[t])
+                nc.scalar.activation(out=tiles[t][:], in_=tiles[t][:], func=ACT.Tanh, scale=scale)
+
+            regroup_after = {0: (5, 0), 1: (5, 1), 2: (6, 0), 3: (6, 1)}
+            quantise_in = {1: 4, 3: 5}
             for t in range(ROW_TILES):
+                big_i, d = pre_i[:, t, :], pre_f[:, t, :]
+                add_input("f", t, d)
+                m_new = recip[:, t, :]
+                nc.vector.scalar_tensor_tensor(out=m_new, in0=d, scalar=0.0, in1=big_i, op0=ALU.max, op1=ALU.add)
+                nc.scalar.activation(out=big_i, in_=d, func=ACT.Exp, scale=-1.0)
+                nc.scalar.activation(out=d, in_=d, func=ACT.Exp)
+                regroup_weight(*regroup_after[t], nc.scalar.copy)
+                nc.sync.dma_start(out=rows_of(m_out, t), in_=m_new)
+                if t in quantise_in:
+                    quantise_weight(quantise_in[t])
+                if t > 0:
+                    n_and_forget(t - 1)
+            n_and_forget(ROW_TILES - 1)
+
+            for half in range(HALVES):
+                regroup_weight(7, half, nc.scalar.copy)
+            nc.scalar.activation(out=recip[:], in_=n_new[:], func=ACT.Ln, bias=N_EPS)
+
+            def reciprocal(t):
                 nc.scalar.activation(
                     out=recip[:, t, :], in_=recip[:, t, :], func=ACT.Exp, bias=math.log(0.5), scale=-1.0
                 )
 
-            recurrent_part("z", lambda t, cols: bias_sb["z"][:, cols])
-            prepare_weights("z")
-            add_input_part("z")
-            for t in range(ROW_TILES):
-                exp_minus_d, f_c, z = pre["i"][:, t, :], pre["f"][:, t, :], pre["z"][:, t, :]
-                nc.scalar.activation(out=z, in_=z, func=ACT.Tanh)
+            def new_cell(t):
+                exp_minus_d, f_c = pre_i[:, t, :], pre_f[:, t, :]
                 nc.vector.scalar_tensor_tensor(
-                    out=z, in0=exp_minus_d, scalar=1.0, in1=z, op0=ALU.min, op1=ALU.mult
+                    out=z[t][:], in0=exp_minus_d, scalar=1.0, in1=z[t][:], op0=ALU.min, op1=ALU.mult
                 )
-                nc.gpsimd.tensor_tensor(out=f_c, in0=f_c, in1=z, op=ALU.add)
+                nc.gpsimd.tensor_tensor(out=f_c, in0=f_c, in1=z[t][:], op=ALU.add)
                 nc.sync.dma_start(out=rows_of(c_out, t), in_=f_c)
                 nc.gpsimd.tensor_tensor(out=recip[:, t, :], in0=recip[:, t, :], in1=f_c, op=ALU.mult)
 
-            recurrent_part("o", lambda t, cols: bias_sb["o"][:, cols])
-            prepare_weights("o")
-            add_input_part("o")
-            for t in range(ROW_TILES):
-                o = pre["o"][:, t, :]
-                nc.scalar.activation(out=o, in_=o, func=ACT.Tanh, scale=0.5)
+            def new_hidden(t):
                 nc.vector.scalar_tensor_tensor(
-                    out=o, in0=o, scalar=1.0, in1=recip[:, t, :], op0=ALU.add, op1=ALU.mult
+                    out=o[t][:], in0=o[t][:], scalar=1.0, in1=recip[:, t, :], op0=ALU.add, op1=ALU.mult
                 )
-                nc.sync.dma_start(out=rows_of(h_out, t), in_=o)
+                nc.sync.dma_start(out=rows_of(h_out, t), in_=o[t][:])
+
+            for t in range(ROW_TILES):
+                z[t] = gate_tile("z")
+                biased_recurrent("z", t, z[t])
+                pre_tanh("z", z, t, 1.0)
+                reciprocal(t)
+            quantise_weight(6)
+            quantise_weight(7)
+            for t in range(ROW_TILES):
+                new_cell(t)
+                o[t] = gate_tile("o")
+                biased_recurrent("o", t, o[t])
+                pre_tanh("o", o, t, 0.5)
+                if t > 1:
+                    new_hidden(t - 2)
+            new_hidden(2)
+            new_hidden(3)

@@ -31,14 +31,6 @@ RAW_AHEAD = 3
 FLOPS = 2 * B * DI * DH * 4 + 2 * B * DH * HD * 4
 
 
-def runs_of_four_out(grouped):
-    return grouped.rearrange("p (c i) t -> p c t i", i=4)
-
-
-def runs_of_four_in(rows):
-    return rows.rearrange("p t (c i) -> p c t i", i=4)
-
-
 def bank_columns(half):
     return slice(half * BANK, (half + 1) * BANK)
 
@@ -94,7 +86,7 @@ def tile_slstmblock_pa_kernel(
 
         def regroup(rows, grouped, half, copy):
             cols = bank_columns(half)
-            copy(out=runs_of_four_out(grouped[:, cols, :]), in_=runs_of_four_in(rows[:, :, cols]))
+            copy(out=grouped[:, cols, :], in_=rows[:, :, cols].rearrange("p t c -> p c t"))
 
         def quantise(grouped, codes, scales, half):
             cols = bank_columns(half)

@@ -67,9 +67,7 @@ def tile_slstmblock_pa_kernel(
         x_scales = state.tile([P, PASSES * B], U8, align_bytes=64)
         h_t = state.tile([P, K_TILES, B], BF16)
         m_sb = state.tile([P, ROW_TILES, DH], BF16)
-        bias_rows = state.tile([P, DH], BF16)
         r_sb = {}
-        bias_sb = {}
 
         chunks = [(gate, g) for gate in GATES for g in range(PASSES)]
         raw_chunk = {}
@@ -120,23 +118,28 @@ def tile_slstmblock_pa_kernel(
         def bank(name):
             return psum.tile([P, BANK], F32, name=name, tag="bank")
 
-        def recurrent_bank(gate, t, half, with_m_and_bias=False):
+        def recurrent_bank(gate, t, half):
             rec = bank("rec")
+            for q in range(BANK // P):
+                c = GATES.index(gate) * K_TILES + half * (BANK // P) + q
+                nc.tensor.matmul(
+                    out=rec[:, q * P : (q + 1) * P], lhsT=b_cols[:, c : c + 1].to_broadcast([P, P]),
+                    rhs=ident_f32[:], is_transpose=True, start=(q == 0), stop=False,
+                )
+            if gate == "f":
+                nc.tensor.matmul(
+                    out=rec[:], lhsT=ident_bf16[:], rhs=m_sb[:, t, bank_columns(half)], start=False, stop=False
+                )
             for hh in range(HEADS_PER_BANK):
                 head = half * HEADS_PER_BANK + hh
-                group = rec[:, hh * HD : (hh + 1) * HD]
-                cols = slice(head * HD, (head + 1) * HD)
-                if with_m_and_bias:
-                    nc.tensor.matmul(out=group, lhsT=ident_bf16[:], rhs=m_sb[:, t, cols], start=True, stop=False)
-                    nc.tensor.matmul(out=group, lhsT=ones[:], rhs=bias_rows[:, cols], start=False, stop=False)
                 for kt in range(K_TILES_PER_HEAD):
                     k_tile = head * K_TILES_PER_HEAD + kt
                     nc.tensor.matmul(
-                        out=group,
+                        out=rec[:, hh * HD : (hh + 1) * HD],
                         lhsT=h_t[:, k_tile, t * P : (t + 1) * P],
                         rhs=r_sb[gate][:, k_tile, :],
-                        start=(kt == 0 and not with_m_and_bias),
-                        stop=(kt == K_TILES_PER_HEAD - 1),
+                        start=False,
+                        stop=(hh == HEADS_PER_BANK - 1 and kt == K_TILES_PER_HEAD - 1),
                     )
             return rec
 
@@ -156,11 +159,10 @@ def tile_slstmblock_pa_kernel(
                 )
             return acc
 
-        def biased_recurrent(gate, t, out):
+        def copy_recurrent(gate, t, out):
             for half in range(HALVES):
-                cols = bank_columns(half)
                 rec = recurrent_bank(gate, t, half)
-                nc.vector.tensor_tensor(out=out[:, cols], in0=rec[:], in1=bias_sb[gate][:, cols], op=ALU.add)
+                nc.scalar.copy(out=out[:, bank_columns(half)], in_=rec[:])
 
         def add_input(gate, t, out):
             for half in range(HALVES):
@@ -176,32 +178,25 @@ def tile_slstmblock_pa_kernel(
             ln_b_raw = early.tile([P, PASSES, PACK], BF16)
             nc.scalar.dma_start(out=ln_w_raw[:], in_=ln_w.rearrange("(g p t) -> p g t", p=P, t=PACK))
             nc.scalar.dma_start(out=ln_b_raw[:], in_=ln_b.rearrange("(g p t) -> p g t", p=P, t=PACK))
-            minus_half = const.tile([P, 1], F32)
-            nc.gpsimd.memset(minus_half[:], -0.5)
-            vec_rows = {}
-
-            def load_bias_rows(name, gates):
-                rows = early.tile([P, P], BF16, name="vec_rows_" + name)
-                nc.gpsimd.memset(rows[:], 0.0)
-                vecs = [biases[gate][0] for gate in gates] + [biases[gate][1] for gate in gates]
-                for v, vec in enumerate(vecs):
-                    nc.gpsimd.dma_start(
-                        out=rows[v * K_TILES : (v + 1) * K_TILES, :], in_=vec.rearrange("(r c) -> r c", c=P)
-                    )
-                vec_rows[name] = rows
-
-            load_bias_rows("i", ("i",))
             start_weight_load(0)
             h_sb = early.tile([P, ROW_TILES, DH], BF16)
             nc.sync.dma_start(out=h_sb[:], in_=by_row_tile(h_prev))
-            start_weight_load(1)
+            vec_rows = early.tile([P, P], BF16)
+            nc.vector.memset(vec_rows[:], 0.0)
+            for v, vec in enumerate([biases[gate][k] for k in range(2) for gate in GATES]):
+                nc.sync.dma_start(
+                    out=vec_rows[v * K_TILES : (v + 1) * K_TILES, :], in_=vec.rearrange("(r c) -> r c", c=P)
+                )
             load_recurrent(early, "i")
+            start_weight_load(1)
             start_weight_load(2)
             load_recurrent(state, "f")
             nc.sync.dma_start(out=m_sb[:], in_=by_row_tile(m_prev))
             load_recurrent(state, "z")
             load_recurrent(state, "o")
 
+            minus_half = const.tile([P, 1], F32)
+            nc.gpsimd.memset(minus_half[:], -0.5)
             warm = const.tile([P, 1], F32)
             nc.scalar.activation(out=warm[:], in_=minus_half[:], func=ACT.Exp)
             ident_f32 = const.tile([P, P], F32)
@@ -238,33 +233,6 @@ def tile_slstmblock_pa_kernel(
 
             ident_bf16 = const.tile([P, P], BF16)
             make_identity(nc, ident_bf16[:])
-            ones = const.tile([P, P], BF16)
-            nc.gpsimd.memset(ones[:], 1.0)
-            load_bias_rows("zo", ("z", "o"))
-            nc.gpsimd.memset(bias_rows[:], 0.0)
-            for r, vec in enumerate(biases["f"]):
-                nc.gpsimd.dma_start(out=bias_rows[r : r + 1, :], in_=vec.rearrange("(o n) -> o n", o=1))
-
-            def bias_columns(name, n_gates):
-                vec_ps = psum.tile([P, P], BF16, name="vec_ps", tag="bank")
-                nc.tensor.transpose(vec_ps[:], vec_rows[name][:], ident_bf16[:])
-                n_cols = n_gates * K_TILES
-                rb_cols = const.tile([P, n_cols], F32, name="rb_cols_" + name)
-                b_cols = const.tile([P, n_cols], F32, name="b_cols_" + name)
-                nc.vector.tensor_copy(out=rb_cols[:], in_=vec_ps[:, n_cols : 2 * n_cols])
-                nc.vector.tensor_tensor(out=b_cols[:], in0=vec_ps[:, 0:n_cols], in1=rb_cols[:], op=ALU.add)
-                return b_cols
-
-            def spread_bias(gate, b_cols, first):
-                bias_sb[gate] = state.tile([P, DH], F32, name="bias_" + gate)
-                for half in range(HALVES):
-                    bias_ps = bank("bias_ps")
-                    for q in range(BANK // P):
-                        c = first + half * (BANK // P) + q
-                        nc.tensor.transpose(
-                            bias_ps[:, q * P : (q + 1) * P], b_cols[:, c : c + 1].to_broadcast([P, P]), ident_f32[:]
-                        )
-                    nc.scalar.copy(out=bias_sb[gate][:, bank_columns(half)], in_=bias_ps[:])
 
             for half in range(HALVES):
                 regroup_weight(0, half, nc.vector.tensor_copy)
@@ -283,11 +251,16 @@ def tile_slstmblock_pa_kernel(
                         bias=ln_cols[:, 8 + r : 9 + r], scale=ln_cols[:, r : r + 1],
                     )
                 if g == 0:
-                    i_cols = bias_columns("i", 1)
+                    vec_ps = psum.tile([P, P], BF16, name="vec_ps", tag="bank")
+                    nc.tensor.transpose(vec_ps[:], vec_rows[:], ident_bf16[:])
+                    n_cols = len(GATES) * K_TILES
+                    rb_cols = const.tile([P, n_cols], F32)
+                    b_cols = const.tile([P, n_cols], F32)
+                    nc.vector.tensor_copy(out=rb_cols[:], in_=vec_ps[:, n_cols : 2 * n_cols])
+                    nc.vector.tensor_tensor(out=b_cols[:], in0=vec_ps[:, 0:n_cols], in1=rb_cols[:], op=ALU.add)
                 regroup(xn_t, x_grouped, g, nc.vector.tensor_copy)
             for g in range(PASSES):
                 quantise(x_grouped, x_codes, x_scales, g)
-            spread_bias("i", i_cols, 0)
 
             for t in range(ROW_TILES):
                 h_ps = psum.tile([P, K_TILES, P], BF16, name="h_ps", tag="bank")
@@ -296,23 +269,20 @@ def tile_slstmblock_pa_kernel(
                 nc.scalar.copy(out=h_t[:, :, t * P : (t + 1) * P], in_=h_ps[:])
 
             for half in range(HALVES):
-                regroup_weight(1, half, nc.scalar.copy)
-            for t in range(ROW_TILES):
-                biased_recurrent("i", t, pre_i[:, t, :])
-            zo_cols = bias_columns("zo", 2)
+                regroup_weight(1, half, nc.vector.tensor_copy)
             quantise_weight(1)
+            for t in range(ROW_TILES):
+                copy_recurrent("i", t, pre_i[:, t, :])
 
         with (
             tc.tile_pool(name="late", bufs=1) as late,
-            tc.tile_pool(name="stream", bufs=5) as stream,
+            tc.tile_pool(name="stream", bufs=9) as stream,
         ):
             n_sb = late.tile([P, ROW_TILES, DH], BF16)
             c_sb = late.tile([P, ROW_TILES, DH], BF16)
             n_new = late.tile([P, ROW_TILES, DH], F32)
             recip = late.tile([P, ROW_TILES, DH], F32)
 
-            spread_bias("z", zo_cols, 0)
-            spread_bias("o", zo_cols, K_TILES)
             for half in range(HALVES):
                 regroup_weight(2, half, nc.scalar.copy)
             nc.sync.dma_start(out=n_sb[:], in_=by_row_tile(n_prev))
@@ -323,7 +293,7 @@ def tile_slstmblock_pa_kernel(
                 regroup_weight(4, half, nc.scalar.copy)
 
             def forget_banks(t):
-                return [recurrent_bank("f", t, half, with_m_and_bias=True) for half in range(HALVES)]
+                return [recurrent_bank("f", t, half) for half in range(HALVES)]
 
             def forget_less_input(t, recs):
                 for half, rec in enumerate(recs):
@@ -356,6 +326,14 @@ def tile_slstmblock_pa_kernel(
                 )
                 nc.sync.dma_start(out=rows_of(n_out, t), in_=n_new[:, t, :])
 
+            def logarithm():
+                nc.scalar.activation(out=recip[:], in_=n_new[:], func=ACT.Ln, bias=N_EPS)
+
+            def reciprocal(t):
+                nc.scalar.activation(
+                    out=recip[:, t, :], in_=recip[:, t, :], func=ACT.Exp, bias=math.log(0.5), scale=-1.0
+                )
+
             def gate_tile(name):
                 return stream.tile([P, DH], F32, name=name, tag="wide")
 
@@ -366,8 +344,14 @@ def tile_slstmblock_pa_kernel(
                 add_input(gate, t, tiles[t])
                 nc.scalar.activation(out=tiles[t][:], in_=tiles[t][:], func=ACT.Tanh, scale=scale)
 
-            regroup_after = {0: (5, 0), 1: (5, 1), 2: (6, 0), 3: (6, 1)}
-            quantise_in = {1: 4, 3: 5}
+            def scalar_regroups(j):
+                for half in range(HALVES):
+                    regroup_weight(j, half, nc.scalar.copy)
+
+            def scalar_copies_recurrent(gate, tiles, t):
+                tiles[t] = gate_tile(gate)
+                copy_recurrent(gate, t, tiles[t])
+
             for t in range(ROW_TILES):
                 big_i, d = pre_i[:, t, :], pre_f[:, t, :]
                 add_input("f", t, d)
@@ -375,31 +359,40 @@ def tile_slstmblock_pa_kernel(
                 nc.vector.scalar_tensor_tensor(out=m_new, in0=d, scalar=0.0, in1=big_i, op0=ALU.max, op1=ALU.add)
                 nc.scalar.activation(out=big_i, in_=d, func=ACT.Exp, scale=-1.0)
                 nc.scalar.activation(out=d, in_=d, func=ACT.Exp)
-                regroup_weight(*regroup_after[t], nc.scalar.copy)
+                if t % 2 == 0:
+                    scalar_regroups(5 + t // 2)
                 nc.sync.dma_start(out=rows_of(m_out, t), in_=m_new)
-                if t in quantise_in:
-                    quantise_weight(quantise_in[t])
+                if t == 1:
+                    quantise_weight(4)
+                if t == 2:
+                    quantise_weight(5)
                 if t > 0:
                     n_and_forget(t - 1)
+                scalar_copies_recurrent("z", z, t)
+            pre_tanh("z", z, 0, 1.0)
+            pre_tanh("z", z, 1, 1.0)
             n_and_forget(ROW_TILES - 1)
-
-            for half in range(HALVES):
-                regroup_weight(7, half, nc.scalar.copy)
-            nc.scalar.activation(out=recip[:], in_=n_new[:], func=ACT.Ln, bias=N_EPS)
-
-            def reciprocal(t):
-                nc.scalar.activation(
-                    out=recip[:, t, :], in_=recip[:, t, :], func=ACT.Exp, bias=math.log(0.5), scale=-1.0
-                )
+            pre_tanh("z", z, 2, 1.0)
+            pre_tanh("z", z, 3, 1.0)
+            scalar_regroups(7)
+            quantise_weight(6)
+            logarithm()
 
             def new_cell(t):
                 exp_minus_d, f_c = pre_i[:, t, :], pre_f[:, t, :]
                 nc.vector.scalar_tensor_tensor(
                     out=z[t][:], in0=exp_minus_d, scalar=1.0, in1=z[t][:], op0=ALU.min, op1=ALU.mult
                 )
-                nc.gpsimd.tensor_tensor(out=f_c, in0=f_c, in1=z[t][:], op=ALU.add)
+                if t > 0:
+                    add_cell(t - 1)
+
+            def add_cell(t):
+                f_c = pre_f[:, t, :]
+                nc.vector.tensor_tensor(out=f_c, in0=f_c, in1=z[t][:], op=ALU.add)
                 nc.sync.dma_start(out=rows_of(c_out, t), in_=f_c)
-                nc.gpsimd.tensor_tensor(out=recip[:, t, :], in0=recip[:, t, :], in1=f_c, op=ALU.mult)
+
+            def cell_over_n(t):
+                nc.vector.tensor_tensor(out=recip[:, t, :], in0=recip[:, t, :], in1=pre_f[:, t, :], op=ALU.mult)
 
             def new_hidden(t):
                 nc.vector.scalar_tensor_tensor(
@@ -408,18 +401,14 @@ def tile_slstmblock_pa_kernel(
                 nc.sync.dma_start(out=rows_of(h_out, t), in_=o[t][:])
 
             for t in range(ROW_TILES):
-                z[t] = gate_tile("z")
-                biased_recurrent("z", t, z[t])
-                pre_tanh("z", z, t, 1.0)
-                reciprocal(t)
-            quantise_weight(6)
-            quantise_weight(7)
-            for t in range(ROW_TILES):
+                scalar_copies_recurrent("o", o, t)
                 new_cell(t)
-                o[t] = gate_tile("o")
-                biased_recurrent("o", t, o[t])
+            quantise_weight(7)
+            add_cell(ROW_TILES - 1)
+            for t in range(ROW_TILES):
+                reciprocal(t)
                 pre_tanh("o", o, t, 0.5)
-                if t > 1:
-                    new_hidden(t - 2)
-            new_hidden(2)
-            new_hidden(3)
+                cell_over_n(t)
+                if t > 0:
+                    new_hidden(t - 1)
+            new_hidden(ROW_TILES - 1)

@@ -58,8 +58,9 @@ def tile_slstmblock_pa_kernel(
         tc.tile_pool(name="state", bufs=1) as state,
         tc.tile_pool(name="w_raw", bufs=RAW_AHEAD) as w_raw,
         tc.tile_pool(name="w_grouped", bufs=3) as w_grouped,
-        tc.tile_pool(name="w_quant", bufs=len(GATES) * PASSES) as w_quant,
-        tc.psum_pool(name="psum", bufs=8) as psum,
+        tc.tile_pool(name="w_quant", bufs=2 * PASSES) as w_quant,
+        tc.tile_pool(name="in_t", bufs=2 * HALVES) as in_pool,
+        tc.psum_pool(name="psum", bufs=4) as psum,
     ):
         pre_i = state.tile([P, ROW_TILES, DH], F32)
         pre_f = state.tile([P, ROW_TILES, DH], F32)
@@ -72,6 +73,7 @@ def tile_slstmblock_pa_kernel(
         chunks = [(gate, g) for gate in GATES for g in range(PASSES)]
         raw_chunk = {}
         grouped_chunk = {}
+        in_halves = {}
         w_codes = {}
         w_scales = {}
 
@@ -94,12 +96,11 @@ def tile_slstmblock_pa_kernel(
                 in_=grouped[:, cols, :].rearrange("p c t -> p (c t)"),
             )
 
-        def regroup_weight(j, half, copy):
-            if half == 0:
+        def regroup_weight(j, copy, halves=(0, 1)):
+            if j not in grouped_chunk:
                 grouped_chunk[j] = w_grouped.tile([P, DH, PACK], BF16, name="grouped", align_bytes=64)
-            regroup(raw_chunk[j], grouped_chunk[j], half, copy)
-            if half == HALVES - 1 and j + RAW_AHEAD < len(chunks):
-                start_weight_load(j + RAW_AHEAD)
+            for half in halves:
+                regroup(raw_chunk[j], grouped_chunk[j], half, copy)
 
         def quantise_weight(j):
             codes = w_quant.tile([P, DH], U32, name="codes", align_bytes=64)
@@ -115,60 +116,58 @@ def tile_slstmblock_pa_kernel(
                 out=r_sb[gate][:], in_=recurrent[gate].rearrange("h (kt p) n -> p (h kt) n", p=P)
             )
 
-        def bank(name):
-            return psum.tile([P, BANK], F32, name=name, tag="bank")
+        def bank(name, tag="acc"):
+            return psum.tile([P, BANK], F32, name=name, tag=tag)
 
-        def recurrent_bank(gate, t, half):
-            rec = bank("rec")
+        def input_half(gate, half, copies):
+            in_t = in_pool.tile([P, BANK // P, B], F32, name="in_t")
+            for q, engine in enumerate(copies):
+                block = half * (BANK // P) + q
+                cols = slice(block * P, (block + 1) * P)
+                acc = bank("acc")
+                for g in range(PASSES):
+                    rows = slice(g * B, (g + 1) * B)
+                    nc.tensor.matmul_mx(
+                        out=acc[:],
+                        lhsT=w_codes[(gate, g)][:, cols].bitcast(FP8X4),
+                        lhsT_scale=w_scales[(gate, g)][:, cols],
+                        rhs=x_codes[:, rows].bitcast(FP8X4),
+                        rhs_scale=x_scales[:, rows],
+                        start=(g == 0),
+                        stop=(g == PASSES - 1),
+                    )
+                c = GATES.index(gate) * K_TILES + block
+                bias = b_cols[:, c : c + 1]
+                if engine == "s":
+                    nc.scalar.activation(out=in_t[:, q, :], in_=acc[:], func=ACT.Identity, bias=bias)
+                else:
+                    nc.vector.tensor_scalar(out=in_t[:, q, :], in0=acc[:], scalar1=bias, scalar2=None, op0=ALU.add)
+            in_halves[(gate, half)] = in_t
+
+        def sum_bank(gate, t, half):
+            total = bank("total", tag="total")
             for q in range(BANK // P):
-                c = GATES.index(gate) * K_TILES + half * (BANK // P) + q
                 nc.tensor.matmul(
-                    out=rec[:, q * P : (q + 1) * P], lhsT=b_cols[:, c : c + 1].to_broadcast([P, P]),
+                    out=total[:, q * P : (q + 1) * P],
+                    lhsT=in_halves[(gate, half)][:, q, t * P : (t + 1) * P],
                     rhs=ident_f32[:], is_transpose=True, start=(q == 0), stop=False,
                 )
             if gate == "f":
                 nc.tensor.matmul(
-                    out=rec[:], lhsT=ident_bf16[:], rhs=m_sb[:, t, bank_columns(half)], start=False, stop=False
+                    out=total[:], lhsT=ident_bf16[:], rhs=m_sb[:, t, bank_columns(half)], start=False, stop=False
                 )
             for hh in range(HEADS_PER_BANK):
                 head = half * HEADS_PER_BANK + hh
                 for kt in range(K_TILES_PER_HEAD):
                     k_tile = head * K_TILES_PER_HEAD + kt
                     nc.tensor.matmul(
-                        out=rec[:, hh * HD : (hh + 1) * HD],
+                        out=total[:, hh * HD : (hh + 1) * HD],
                         lhsT=h_t[:, k_tile, t * P : (t + 1) * P],
                         rhs=r_sb[gate][:, k_tile, :],
                         start=False,
                         stop=(hh == HEADS_PER_BANK - 1 and kt == K_TILES_PER_HEAD - 1),
                     )
-            return rec
-
-        def input_bank(gate, t, half):
-            cols = bank_columns(half)
-            acc = bank("acc")
-            for g in range(PASSES):
-                rows = slice(g * B + t * P, g * B + (t + 1) * P)
-                nc.tensor.matmul_mx(
-                    out=acc[:],
-                    lhsT=x_codes[:, rows].bitcast(FP8X4),
-                    lhsT_scale=x_scales[:, rows],
-                    rhs=w_codes[(gate, g)][:, cols].bitcast(FP8X4),
-                    rhs_scale=w_scales[(gate, g)][:, cols],
-                    start=(g == 0),
-                    stop=(g == PASSES - 1),
-                )
-            return acc
-
-        def copy_recurrent(gate, t, out):
-            for half in range(HALVES):
-                rec = recurrent_bank(gate, t, half)
-                nc.scalar.copy(out=out[:, bank_columns(half)], in_=rec[:])
-
-        def add_input(gate, t, out):
-            for half in range(HALVES):
-                cols = bank_columns(half)
-                acc = input_bank(gate, t, half)
-                nc.vector.tensor_tensor(out=out[:, cols], in0=acc[:], in1=out[:, cols], op=ALU.add)
+            return total
 
         with tc.tile_pool(name="early", bufs=1) as early:
             x_sb = early.tile([P, ROW_TILES, DI], BF16)
@@ -178,18 +177,25 @@ def tile_slstmblock_pa_kernel(
             ln_b_raw = early.tile([P, PASSES, PACK], BF16)
             nc.scalar.dma_start(out=ln_w_raw[:], in_=ln_w.rearrange("(g p t) -> p g t", p=P, t=PACK))
             nc.scalar.dma_start(out=ln_b_raw[:], in_=ln_b.rearrange("(g p t) -> p g t", p=P, t=PACK))
-            start_weight_load(0)
             h_sb = early.tile([P, ROW_TILES, DH], BF16)
             nc.sync.dma_start(out=h_sb[:], in_=by_row_tile(h_prev))
             vec_rows = early.tile([P, P], BF16)
             nc.vector.memset(vec_rows[:], 0.0)
-            for v, vec in enumerate([biases[gate][k] for k in range(2) for gate in GATES]):
+            vecs = [biases[gate][k] for k in range(2) for gate in GATES]
+
+            def load_bias(v):
                 nc.sync.dma_start(
-                    out=vec_rows[v * K_TILES : (v + 1) * K_TILES, :], in_=vec.rearrange("(r c) -> r c", c=P)
+                    out=vec_rows[v * K_TILES : (v + 1) * K_TILES, :], in_=vecs[v].rearrange("(r c) -> r c", c=P)
                 )
-            load_recurrent(early, "i")
+
+            for v in range(4):
+                load_bias(v)
+            start_weight_load(0)
+            for v in range(4, 8):
+                load_bias(v)
             start_weight_load(1)
             start_weight_load(2)
+            load_recurrent(state, "i")
             load_recurrent(state, "f")
             nc.sync.dma_start(out=m_sb[:], in_=by_row_tile(m_prev))
             load_recurrent(state, "z")
@@ -199,44 +205,87 @@ def tile_slstmblock_pa_kernel(
             nc.gpsimd.memset(minus_half[:], -0.5)
             warm = const.tile([P, 1], F32)
             nc.scalar.activation(out=warm[:], in_=minus_half[:], func=ACT.Exp)
-            ident_f32 = const.tile([P, P], F32)
-            make_identity(nc, ident_f32[:])
+            ident_bf16 = const.tile([P, P], BF16)
+            make_identity(nc, ident_bf16[:])
 
-            stats = early.tile([P, ROW_TILES, 2, 6], F32)
-            mean_var = early.tile([P, ROW_TILES, 2], F32)
-            minus_mean = early.tile([P, ROW_TILES], F32)
+            stats = early.tile([P, 2, 2, 6], F32)
+            sums = early.tile([P, ROW_TILES, 2], F32)
+            mean_var = early.tile([P, 2, 2], F32)
+            scalar_mean = early.tile([P, ROW_TILES], F32)
             var_eps = early.tile([P, ROW_TILES], F32)
             rstd = early.tile([P, ROW_TILES], F32)
-            shift = early.tile([P, ROW_TILES], F32)
             y = early.tile([P, ROW_TILES, DI], F32)
-            for t in range(ROW_TILES):
-                one = slice(t, t + 1)
+
+            def vector_statistics(t):
                 for s in range(2):
                     nc.vector.bn_stats(out=stats[:, t, s, :], in_=x_sb[:, t, s * 512 : (s + 1) * 512])
                 nc.vector.bn_aggr(out=mean_var[:, t, :], in_=stats[:, t, :, :].rearrange("p s f -> p (s f)"))
                 nc.gpsimd.tensor_scalar(
-                    out=var_eps[:, one], in0=mean_var[:, t, 1:2], scalar1=LN_EPS, scalar2=None, op0=ALU.add
+                    out=var_eps[:, t : t + 1], in0=mean_var[:, t, 1:2], scalar1=LN_EPS, scalar2=None, op0=ALU.add
                 )
-                nc.gpsimd.tensor_tensor(out=rstd[:, one], in0=var_eps[:, one], in1=minus_half[:], op=ALU.pow)
+
+            def scalar_sum(t):
+                nc.scalar.activation(out=y[:, t, :], in_=x_sb[:, t, :], func=ACT.Identity, accum_out=sums[:, t, 0:1])
                 nc.gpsimd.tensor_scalar(
-                    out=minus_mean[:, one], in0=mean_var[:, t, 0:1], scalar1=-1.0, scalar2=None, op0=ALU.mult
+                    out=scalar_mean[:, t : t + 1], in0=sums[:, t, 0:1], scalar1=1.0 / DI, scalar2=None, op0=ALU.mult
                 )
-                nc.gpsimd.tensor_tensor(out=shift[:, one], in0=minus_mean[:, one], in1=rstd[:, one], op=ALU.mult)
+
+            def scalar_squares(t):
                 nc.scalar.activation(
-                    out=y[:, t, :].rearrange("b (g j p) -> b g j p", j=PACK, p=P),
-                    in_=x_sb[:, t, :].rearrange("b (g p j) -> b g j p", j=PACK, p=P),
-                    func=ACT.Identity, bias=shift[:, one], scale=rstd[:, one],
+                    out=y[:, t, :], in_=x_sb[:, t, :], func=ACT.Square, scale=-1.0, bias=scalar_mean[:, t : t + 1],
+                    accum_out=sums[:, t, 1:2],
                 )
+                nc.gpsimd.tensor_scalar(
+                    out=var_eps[:, t : t + 1], in0=sums[:, t, 1:2], scalar1=1.0 / DI, scalar2=LN_EPS,
+                    op0=ALU.mult, op1=ALU.add,
+                )
+
+            def normalise(t):
+                mean = mean_var[:, t, 0:1] if t < 2 else scalar_mean[:, t : t + 1]
+                nc.gpsimd.tensor_tensor(
+                    out=rstd[:, t : t + 1], in0=var_eps[:, t : t + 1], in1=minus_half[:], op=ALU.pow
+                )
+                nc.vector.tensor_scalar(
+                    out=y[:, t, :].rearrange("b (g j p) -> b g j p", j=PACK, p=P),
+                    in0=x_sb[:, t, :].rearrange("b (g p j) -> b g j p", j=PACK, p=P),
+                    scalar1=mean, scalar2=rstd[:, t : t + 1], op0=ALU.subtract, op1=ALU.mult,
+                )
+
+            vector_statistics(0)
+            scalar_sum(2)
+            scalar_sum(3)
+            vector_statistics(1)
             ln_cols = early.tile([P, 2 * PASSES * PACK], F32)
             nc.vector.tensor_copy(out=ln_cols[:, 0:8], in_=ln_w_raw[:].rearrange("p g t -> p (g t)"))
             nc.vector.tensor_copy(out=ln_cols[:, 8:16], in_=ln_b_raw[:].rearrange("p g t -> p (g t)"))
+            normalise(0)
+            scalar_squares(2)
+            normalise(1)
+            scalar_squares(3)
+            normalise(2)
+            normalise(3)
+            ident_f32 = const.tile([P, P], F32)
+            make_identity(nc, ident_f32[:])
 
-            ident_bf16 = const.tile([P, P], BF16)
-            make_identity(nc, ident_bf16[:])
+            def transpose_h(t):
+                h_ps = psum.tile([P, K_TILES, P], BF16, name="h_ps", tag="acc")
+                for kt in range(K_TILES):
+                    nc.tensor.transpose(h_ps[:, kt, :], h_sb[:, t, kt * P : (kt + 1) * P], ident_bf16[:])
+                nc.vector.tensor_copy(out=h_t[:, :, t * P : (t + 1) * P], in_=h_ps[:])
 
-            for half in range(HALVES):
-                regroup_weight(0, half, nc.vector.tensor_copy)
-            quantise_weight(0)
+            transpose_h(0)
+            transpose_h(1)
+
+            vec_ps = psum.tile([P, P], BF16, name="vec_ps", tag="acc")
+            nc.tensor.transpose(vec_ps[:], vec_rows[:], ident_bf16[:])
+            n_cols = len(GATES) * K_TILES
+            rb_cols = const.tile([P, n_cols], F32)
+            b_cols = const.tile([P, n_cols], F32)
+            nc.vector.tensor_copy(out=rb_cols[:], in_=vec_ps[:, n_cols : 2 * n_cols])
+            nc.vector.tensor_tensor(out=b_cols[:], in0=vec_ps[:, 0:n_cols], in1=rb_cols[:], op=ALU.add)
+
+            regroup_weight(0, nc.vector.tensor_copy)
+            start_weight_load(3)
 
             xn_t = early.tile([P, PACK, PASSES * B], BF16)
             x_grouped = w_grouped.tile([P, PASSES * B, PACK], BF16, name="grouped", align_bytes=64)
@@ -250,70 +299,47 @@ def tile_slstmblock_pa_kernel(
                         out=xn_t[:, t4, g * B : (g + 1) * B], in_=y_ps[:], func=ACT.Identity,
                         bias=ln_cols[:, 8 + r : 9 + r], scale=ln_cols[:, r : r + 1],
                     )
-                if g == 0:
-                    vec_ps = psum.tile([P, P], BF16, name="vec_ps", tag="bank")
-                    nc.tensor.transpose(vec_ps[:], vec_rows[:], ident_bf16[:])
-                    n_cols = len(GATES) * K_TILES
-                    rb_cols = const.tile([P, n_cols], F32)
-                    b_cols = const.tile([P, n_cols], F32)
-                    nc.vector.tensor_copy(out=rb_cols[:], in_=vec_ps[:, n_cols : 2 * n_cols])
-                    nc.vector.tensor_tensor(out=b_cols[:], in0=vec_ps[:, 0:n_cols], in1=rb_cols[:], op=ALU.add)
                 regroup(xn_t, x_grouped, g, nc.vector.tensor_copy)
+                if g == 0:
+                    quantise_weight(0)
+            regroup_weight(1, nc.vector.tensor_copy, (0,))
             for g in range(PASSES):
                 quantise(x_grouped, x_codes, x_scales, g)
 
-            for t in range(ROW_TILES):
-                h_ps = psum.tile([P, K_TILES, P], BF16, name="h_ps", tag="bank")
-                for kt in range(K_TILES):
-                    nc.tensor.transpose(h_ps[:, kt, :], h_sb[:, t, kt * P : (kt + 1) * P], ident_bf16[:])
-                nc.scalar.copy(out=h_t[:, :, t * P : (t + 1) * P], in_=h_ps[:])
-
-            for half in range(HALVES):
-                regroup_weight(1, half, nc.vector.tensor_copy)
+            regroup_weight(1, nc.scalar.copy, (1,))
+            start_weight_load(4)
             quantise_weight(1)
-            for t in range(ROW_TILES):
-                copy_recurrent("i", t, pre_i[:, t, :])
+            regroup_weight(2, nc.scalar.copy, (1,))
+            transpose_h(2)
+            transpose_h(3)
 
         with (
             tc.tile_pool(name="late", bufs=1) as late,
-            tc.tile_pool(name="stream", bufs=9) as stream,
+            tc.tile_pool(name="stream", bufs=ROW_TILES) as stream,
         ):
             n_sb = late.tile([P, ROW_TILES, DH], BF16)
             c_sb = late.tile([P, ROW_TILES, DH], BF16)
             n_new = late.tile([P, ROW_TILES, DH], F32)
             recip = late.tile([P, ROW_TILES, DH], F32)
+            z = {}
 
-            for half in range(HALVES):
-                regroup_weight(2, half, nc.scalar.copy)
-            nc.sync.dma_start(out=n_sb[:], in_=by_row_tile(n_prev))
-            nc.sync.dma_start(out=c_sb[:], in_=by_row_tile(c_prev))
-            for half in range(HALVES):
-                regroup_weight(3, half, nc.scalar.copy)
-            for half in range(HALVES):
-                regroup_weight(4, half, nc.scalar.copy)
+            def input_gate(t, copy):
+                for half in range(HALVES):
+                    copy(out=pre_i[:, t, bank_columns(half)], in_=sum_bank("i", t, half)[:])
 
-            def forget_banks(t):
-                return [recurrent_bank("f", t, half) for half in range(HALVES)]
-
-            def forget_less_input(t, recs):
-                for half, rec in enumerate(recs):
+            def stabiliser(t):
+                big_i, d = pre_i[:, t, :], pre_f[:, t, :]
+                for half in range(HALVES):
                     cols = bank_columns(half)
-                    nc.vector.tensor_tensor(
-                        out=pre_f[:, t, cols], in0=rec[:], in1=pre_i[:, t, cols], op=ALU.subtract
-                    )
+                    total = sum_bank("f", t, half)
+                    nc.vector.tensor_tensor(out=d[:, cols], in0=total[:], in1=big_i[:, cols], op=ALU.subtract)
+                m_new = recip[:, t, :]
+                nc.vector.scalar_tensor_tensor(out=m_new, in0=d, scalar=0.0, in1=big_i, op0=ALU.max, op1=ALU.add)
+                nc.scalar.activation(out=big_i, in_=d, func=ACT.Exp, scale=-1.0)
+                nc.scalar.activation(out=d, in_=d, func=ACT.Exp)
+                nc.sync.dma_start(out=rows_of(m_out, t), in_=m_new)
 
-            recs = {}
-            for t in range(ROW_TILES):
-                add_input("i", t, pre_i[:, t, :])
-                recs[t] = forget_banks(t)
-                if t > 0:
-                    forget_less_input(t - 1, recs[t - 1])
-                if t == 1:
-                    quantise_weight(2)
-            forget_less_input(ROW_TILES - 1, recs[ROW_TILES - 1])
-            quantise_weight(3)
-
-            def n_and_forget(t):
+            def normaliser(t):
                 exp_minus_d, exp_d = pre_i[:, t, :], pre_f[:, t, :]
                 nc.vector.scalar_tensor_tensor(
                     out=n_new[:, t, :], in0=exp_d, scalar=1.0, in1=n_sb[:, t, :], op0=ALU.min, op1=ALU.mult
@@ -326,6 +352,19 @@ def tile_slstmblock_pa_kernel(
                 )
                 nc.sync.dma_start(out=rows_of(n_out, t), in_=n_new[:, t, :])
 
+            def tanh_gate(gate, t, out, scale):
+                for half in range(HALVES):
+                    nc.scalar.activation(
+                        out=out[:, bank_columns(half)], in_=sum_bank(gate, t, half)[:], func=ACT.Tanh, scale=scale
+                    )
+
+            def cell_input(t):
+                z[t] = stream.tile([P, DH], F32, name="z")
+                tanh_gate("z", t, z[t], 1.0)
+
+            def output_gate(t):
+                tanh_gate("o", t, pre_i[:, t, :], 0.5)
+
             def logarithm():
                 nc.scalar.activation(out=recip[:], in_=n_new[:], func=ACT.Ln, bias=N_EPS)
 
@@ -334,59 +373,12 @@ def tile_slstmblock_pa_kernel(
                     out=recip[:, t, :], in_=recip[:, t, :], func=ACT.Exp, bias=math.log(0.5), scale=-1.0
                 )
 
-            def gate_tile(name):
-                return stream.tile([P, DH], F32, name=name, tag="wide")
-
-            z = {}
-            o = {}
-
-            def pre_tanh(gate, tiles, t, scale):
-                add_input(gate, t, tiles[t])
-                nc.scalar.activation(out=tiles[t][:], in_=tiles[t][:], func=ACT.Tanh, scale=scale)
-
-            def scalar_regroups(j):
-                for half in range(HALVES):
-                    regroup_weight(j, half, nc.scalar.copy)
-
-            def scalar_copies_recurrent(gate, tiles, t):
-                tiles[t] = gate_tile(gate)
-                copy_recurrent(gate, t, tiles[t])
-
-            for t in range(ROW_TILES):
-                big_i, d = pre_i[:, t, :], pre_f[:, t, :]
-                add_input("f", t, d)
-                m_new = recip[:, t, :]
-                nc.vector.scalar_tensor_tensor(out=m_new, in0=d, scalar=0.0, in1=big_i, op0=ALU.max, op1=ALU.add)
-                nc.scalar.activation(out=big_i, in_=d, func=ACT.Exp, scale=-1.0)
-                nc.scalar.activation(out=d, in_=d, func=ACT.Exp)
-                if t % 2 == 0:
-                    scalar_regroups(5 + t // 2)
-                nc.sync.dma_start(out=rows_of(m_out, t), in_=m_new)
-                if t == 1:
-                    quantise_weight(4)
-                if t == 2:
-                    quantise_weight(5)
-                if t > 0:
-                    n_and_forget(t - 1)
-                scalar_copies_recurrent("z", z, t)
-            pre_tanh("z", z, 0, 1.0)
-            pre_tanh("z", z, 1, 1.0)
-            n_and_forget(ROW_TILES - 1)
-            pre_tanh("z", z, 2, 1.0)
-            pre_tanh("z", z, 3, 1.0)
-            scalar_regroups(7)
-            quantise_weight(6)
-            logarithm()
+            def gated_input(t):
+                nc.vector.scalar_tensor_tensor(
+                    out=z[t][:], in0=pre_i[:, t, :], scalar=1.0, in1=z[t][:], op0=ALU.min, op1=ALU.mult
+                )
 
             def new_cell(t):
-                exp_minus_d, f_c = pre_i[:, t, :], pre_f[:, t, :]
-                nc.vector.scalar_tensor_tensor(
-                    out=z[t][:], in0=exp_minus_d, scalar=1.0, in1=z[t][:], op0=ALU.min, op1=ALU.mult
-                )
-                if t > 0:
-                    add_cell(t - 1)
-
-            def add_cell(t):
                 f_c = pre_f[:, t, :]
                 nc.vector.tensor_tensor(out=f_c, in0=f_c, in1=z[t][:], op=ALU.add)
                 nc.sync.dma_start(out=rows_of(c_out, t), in_=f_c)
@@ -396,19 +388,75 @@ def tile_slstmblock_pa_kernel(
 
             def new_hidden(t):
                 nc.vector.scalar_tensor_tensor(
-                    out=o[t][:], in0=o[t][:], scalar=1.0, in1=recip[:, t, :], op0=ALU.add, op1=ALU.mult
+                    out=recip[:, t, :], in0=pre_i[:, t, :], scalar=1.0, in1=recip[:, t, :], op0=ALU.add, op1=ALU.mult
                 )
-                nc.sync.dma_start(out=rows_of(h_out, t), in_=o[t][:])
+                nc.sync.dma_start(out=rows_of(h_out, t), in_=recip[:, t, :])
 
-            for t in range(ROW_TILES):
-                scalar_copies_recurrent("o", o, t)
-                new_cell(t)
+            ALL_S, ALL_V = "ssss", "vvvv"
+            input_half("i", 0, ALL_S)
+            input_half("i", 1, ALL_S)
+            regroup_weight(2, nc.vector.tensor_copy, (0,))
+            start_weight_load(5)
+            regroup_weight(3, nc.vector.tensor_copy)
+            start_weight_load(6)
+            quantise_weight(2)
+            quantise_weight(3)
+            nc.sync.dma_start(out=n_sb[:], in_=by_row_tile(n_prev))
+            nc.sync.dma_start(out=c_sb[:], in_=by_row_tile(c_prev))
+            input_gate(0, nc.scalar.copy)
+            input_half("f", 0, ALL_S)
+            input_half("f", 1, ALL_S)
+            input_gate(1, nc.scalar.copy)
+            regroup_weight(4, nc.vector.tensor_copy)
+            start_weight_load(7)
+            regroup_weight(5, nc.vector.tensor_copy)
+            quantise_weight(4)
+            quantise_weight(5)
+            regroup_weight(6, nc.scalar.copy, (0,))
+            stabiliser(0)
+            regroup_weight(7, nc.vector.tensor_copy)
+            input_gate(2, nc.scalar.copy)
+            regroup_weight(6, nc.scalar.copy, (1,))
+            input_gate(3, nc.scalar.copy)
+            quantise_weight(6)
+            stabiliser(1)
             quantise_weight(7)
-            add_cell(ROW_TILES - 1)
-            for t in range(ROW_TILES):
-                reciprocal(t)
-                pre_tanh("o", o, t, 0.5)
-                cell_over_n(t)
-                if t > 0:
-                    new_hidden(t - 1)
-            new_hidden(ROW_TILES - 1)
+            input_half("z", 0, ALL_S)
+            normaliser(0)
+            stabiliser(2)
+            input_half("z", 1, ALL_S)
+            normaliser(1)
+            stabiliser(3)
+            input_half("o", 0, ALL_S)
+            cell_input(0)
+            normaliser(2)
+            cell_input(1)
+            normaliser(3)
+            logarithm()
+            gated_input(0)
+            gated_input(1)
+            new_cell(0)
+            new_cell(1)
+            cell_input(2)
+            cell_input(3)
+            input_half("o", 1, ALL_V)
+            reciprocal(0)
+            gated_input(2)
+            gated_input(3)
+            output_gate(0)
+            new_cell(2)
+            new_cell(3)
+            cell_over_n(0)
+            reciprocal(1)
+            output_gate(1)
+            new_hidden(0)
+            cell_over_n(1)
+            reciprocal(2)
+            output_gate(2)
+            new_hidden(1)
+            cell_over_n(2)
+            reciprocal(3)
+            output_gate(3)
+            new_hidden(2)
+            cell_over_n(3)
+            new_hidden(3)

@@ -102,13 +102,13 @@ def tile_slstmblock_pa_kernel(
             for half in halves:
                 regroup(raw_chunk[j], grouped_chunk[j], half, copy)
 
-        def quantise_weight(j):
-            codes = w_quant.tile([P, DH], U32, name="codes", align_bytes=64)
-            scales = w_quant.tile([P, DH], U8, name="scales", align_bytes=64)
-            for half in range(HALVES):
-                quantise(grouped_chunk[j], codes, scales, half)
-            w_codes[chunks[j]] = codes
-            w_scales[chunks[j]] = scales
+        def quantise_weight(j, halves=(0, 1)):
+            key = chunks[j]
+            if key not in w_codes:
+                w_codes[key] = w_quant.tile([P, DH], U32, name="codes", align_bytes=64)
+                w_scales[key] = w_quant.tile([P, DH], U8, name="scales", align_bytes=64)
+            for half in halves:
+                quantise(grouped_chunk[j], w_codes[key], w_scales[key], half)
 
         def load_recurrent(pool, gate):
             r_sb[gate] = pool.tile([P, K_TILES, HD], BF16, name="r_" + gate)
@@ -168,6 +168,9 @@ def tile_slstmblock_pa_kernel(
                         stop=(hh == HEADS_PER_BANK - 1 and kt == K_TILES_PER_HEAD - 1),
                     )
             return total
+
+        def sum_banks(gate, t):
+            return (sum_bank(gate, t, half) for half in range(HALVES))
 
         with tc.tile_pool(name="early", bufs=1) as early:
             x_sb = early.tile([P, ROW_TILES, DI], BF16)
@@ -267,14 +270,45 @@ def tile_slstmblock_pa_kernel(
             ident_f32 = const.tile([P, P], F32)
             make_identity(nc, ident_f32[:])
 
-            def transpose_h(t):
+            def transpose_h(t, copy):
                 h_ps = psum.tile([P, K_TILES, P], BF16, name="h_ps", tag="acc")
                 for kt in range(K_TILES):
                     nc.tensor.transpose(h_ps[:, kt, :], h_sb[:, t, kt * P : (kt + 1) * P], ident_bf16[:])
-                nc.vector.tensor_copy(out=h_t[:, :, t * P : (t + 1) * P], in_=h_ps[:])
+                copy(out=h_t[:, :, t * P : (t + 1) * P], in_=h_ps[:])
 
-            transpose_h(0)
-            transpose_h(1)
+            transpose_h(0, nc.scalar.copy)
+            transpose_h(1, nc.scalar.copy)
+            regroup_weight(0, nc.vector.tensor_copy)
+            start_weight_load(3)
+
+            xn_t = early.tile([P, PACK, PASSES * B], BF16)
+            x_grouped = w_grouped.tile([P, PASSES * B, PACK], BF16, name="grouped", align_bytes=64)
+
+            def normed(g, t4, engine):
+                r = g * PACK + t4
+                y_ps = bank("y_ps")
+                for t in range(ROW_TILES):
+                    nc.tensor.transpose(y_ps[:, t * P : (t + 1) * P], y[:, t, r * P : (r + 1) * P], ident_f32[:])
+                out = xn_t[:, t4, g * B : (g + 1) * B]
+                gain, offset = ln_cols[:, r : r + 1], ln_cols[:, 8 + r : 9 + r]
+                if engine == "s":
+                    nc.scalar.activation(out=out, in_=y_ps[:], func=ACT.Identity, bias=offset, scale=gain)
+                else:
+                    nc.vector.tensor_scalar(
+                        out=out, in0=y_ps[:], scalar1=gain, scalar2=offset, op0=ALU.mult, op1=ALU.add
+                    )
+
+            for t4 in range(PACK):
+                normed(0, t4, "s")
+            regroup(xn_t, x_grouped, 0, nc.vector.tensor_copy)
+            quantise_weight(0, (0,))
+            regroup_weight(1, nc.vector.tensor_copy, (0,))
+            for t4 in range(PACK):
+                normed(1, t4, "s" if t4 < PACK - 1 else "v")
+            quantise_weight(1, (0,))
+            regroup(xn_t, x_grouped, 1, nc.vector.tensor_copy)
+            for g in range(PASSES):
+                quantise(x_grouped, x_codes, x_scales, g)
 
             vec_ps = psum.tile([P, P], BF16, name="vec_ps", tag="acc")
             nc.tensor.transpose(vec_ps[:], vec_rows[:], ident_bf16[:])
@@ -284,34 +318,13 @@ def tile_slstmblock_pa_kernel(
             nc.vector.tensor_copy(out=rb_cols[:], in_=vec_ps[:, n_cols : 2 * n_cols])
             nc.vector.tensor_tensor(out=b_cols[:], in0=vec_ps[:, 0:n_cols], in1=rb_cols[:], op=ALU.add)
 
-            regroup_weight(0, nc.vector.tensor_copy)
-            start_weight_load(3)
-
-            xn_t = early.tile([P, PACK, PASSES * B], BF16)
-            x_grouped = w_grouped.tile([P, PASSES * B, PACK], BF16, name="grouped", align_bytes=64)
-            for g in range(PASSES):
-                for t4 in range(PACK):
-                    r = g * PACK + t4
-                    y_ps = bank("y_ps")
-                    for t in range(ROW_TILES):
-                        nc.tensor.transpose(y_ps[:, t * P : (t + 1) * P], y[:, t, r * P : (r + 1) * P], ident_f32[:])
-                    nc.scalar.activation(
-                        out=xn_t[:, t4, g * B : (g + 1) * B], in_=y_ps[:], func=ACT.Identity,
-                        bias=ln_cols[:, 8 + r : 9 + r], scale=ln_cols[:, r : r + 1],
-                    )
-                regroup(xn_t, x_grouped, g, nc.vector.tensor_copy)
-                if g == 0:
-                    quantise_weight(0)
-            regroup_weight(1, nc.vector.tensor_copy, (0,))
-            for g in range(PASSES):
-                quantise(x_grouped, x_codes, x_scales, g)
-
             regroup_weight(1, nc.scalar.copy, (1,))
             start_weight_load(4)
-            quantise_weight(1)
             regroup_weight(2, nc.scalar.copy, (1,))
-            transpose_h(2)
-            transpose_h(3)
+            quantise_weight(0, (1,))
+            quantise_weight(1, (1,))
+            transpose_h(2, nc.vector.tensor_copy)
+            transpose_h(3, nc.vector.tensor_copy)
 
         with (
             tc.tile_pool(name="late", bufs=1) as late,
@@ -324,14 +337,13 @@ def tile_slstmblock_pa_kernel(
             z = {}
 
             def input_gate(t, copy):
-                for half in range(HALVES):
-                    copy(out=pre_i[:, t, bank_columns(half)], in_=sum_bank("i", t, half)[:])
+                for half, total in enumerate(sum_banks("i", t)):
+                    copy(out=pre_i[:, t, bank_columns(half)], in_=total[:])
 
             def stabiliser(t):
                 big_i, d = pre_i[:, t, :], pre_f[:, t, :]
-                for half in range(HALVES):
+                for half, total in enumerate(sum_banks("f", t)):
                     cols = bank_columns(half)
-                    total = sum_bank("f", t, half)
                     nc.vector.tensor_tensor(out=d[:, cols], in0=total[:], in1=big_i[:, cols], op=ALU.subtract)
                 m_new = recip[:, t, :]
                 nc.vector.scalar_tensor_tensor(out=m_new, in0=d, scalar=0.0, in1=big_i, op0=ALU.max, op1=ALU.add)
@@ -353,10 +365,8 @@ def tile_slstmblock_pa_kernel(
                 nc.sync.dma_start(out=rows_of(n_out, t), in_=n_new[:, t, :])
 
             def tanh_gate(gate, t, out, scale):
-                for half in range(HALVES):
-                    nc.scalar.activation(
-                        out=out[:, bank_columns(half)], in_=sum_bank(gate, t, half)[:], func=ACT.Tanh, scale=scale
-                    )
+                for half, total in enumerate(sum_banks(gate, t)):
+                    nc.scalar.activation(out=out[:, bank_columns(half)], in_=total[:], func=ACT.Tanh, scale=scale)
 
             def cell_input(t):
                 z[t] = stream.tile([P, DH], F32, name="z")
@@ -414,49 +424,49 @@ def tile_slstmblock_pa_kernel(
             quantise_weight(5)
             regroup_weight(6, nc.scalar.copy, (0,))
             stabiliser(0)
-            regroup_weight(7, nc.vector.tensor_copy)
+            stabiliser(1)
             input_gate(2, nc.scalar.copy)
+            regroup_weight(7, nc.vector.tensor_copy)
+            quantise_weight(7)
             regroup_weight(6, nc.scalar.copy, (1,))
             input_gate(3, nc.scalar.copy)
-            quantise_weight(6)
-            stabiliser(1)
-            quantise_weight(7)
             input_half("z", 0, ALL_S)
             normaliser(0)
+            quantise_weight(6)
             stabiliser(2)
             input_half("z", 1, ALL_S)
             normaliser(1)
             stabiliser(3)
-            input_half("o", 0, ALL_S)
             cell_input(0)
             normaliser(2)
             cell_input(1)
-            normaliser(3)
-            logarithm()
+            cell_input(2)
+            cell_input(3)
             gated_input(0)
+            normaliser(3)
+            input_half("o", 0, ALL_S)
+            logarithm()
             gated_input(1)
             new_cell(0)
             new_cell(1)
-            cell_input(2)
-            cell_input(3)
             input_half("o", 1, ALL_V)
-            reciprocal(0)
             gated_input(2)
             gated_input(3)
+            reciprocal(0)
             output_gate(0)
             new_cell(2)
-            new_cell(3)
-            cell_over_n(0)
             reciprocal(1)
+            new_cell(3)
             output_gate(1)
-            new_hidden(0)
-            cell_over_n(1)
+            cell_over_n(0)
             reciprocal(2)
             output_gate(2)
-            new_hidden(1)
-            cell_over_n(2)
+            new_hidden(0)
+            cell_over_n(1)
             reciprocal(3)
             output_gate(3)
-            new_hidden(2)
+            new_hidden(1)
+            cell_over_n(2)
             cell_over_n(3)
+            new_hidden(2)
             new_hidden(3)

@@ -210,6 +210,8 @@ def tile_slstmblock_pa_kernel(
             nc.scalar.activation(out=warm[:], in_=minus_half[:], func=ACT.Exp)
             ident_bf16 = const.tile([P, P], BF16)
             make_identity(nc, ident_bf16[:])
+            ident_f32 = const.tile([P, P], F32)
+            make_identity(nc, ident_f32[:])
 
             stats = early.tile([P, 2, 2, 6], F32)
             sums = early.tile([P, ROW_TILES, 2], F32)
@@ -243,11 +245,13 @@ def tile_slstmblock_pa_kernel(
                     op0=ALU.mult, op1=ALU.add,
                 )
 
-            def normalise(t):
-                mean = mean_var[:, t, 0:1] if t < 2 else scalar_mean[:, t : t + 1]
+            def inverse_deviation(t):
                 nc.gpsimd.tensor_tensor(
                     out=rstd[:, t : t + 1], in0=var_eps[:, t : t + 1], in1=minus_half[:], op=ALU.pow
                 )
+
+            def normalise(t):
+                mean = mean_var[:, t, 0:1] if t < 2 else scalar_mean[:, t : t + 1]
                 nc.vector.tensor_scalar(
                     out=y[:, t, :].rearrange("b (g j p) -> b g j p", j=PACK, p=P),
                     in0=x_sb[:, t, :].rearrange("b (g p j) -> b g j p", j=PACK, p=P),
@@ -255,20 +259,22 @@ def tile_slstmblock_pa_kernel(
                 )
 
             vector_statistics(0)
+            inverse_deviation(0)
             scalar_sum(2)
-            scalar_sum(3)
             vector_statistics(1)
+            inverse_deviation(1)
+            scalar_sum(3)
             ln_cols = early.tile([P, 2 * PASSES * PACK], F32)
             nc.vector.tensor_copy(out=ln_cols[:, 0:8], in_=ln_w_raw[:].rearrange("p g t -> p (g t)"))
             nc.vector.tensor_copy(out=ln_cols[:, 8:16], in_=ln_b_raw[:].rearrange("p g t -> p (g t)"))
             normalise(0)
-            scalar_squares(2)
             normalise(1)
-            scalar_squares(3)
+            scalar_squares(2)
+            inverse_deviation(2)
             normalise(2)
+            scalar_squares(3)
+            inverse_deviation(3)
             normalise(3)
-            ident_f32 = const.tile([P, P], F32)
-            make_identity(nc, ident_f32[:])
 
             def transpose_h(t, copy):
                 h_ps = psum.tile([P, K_TILES, P], BF16, name="h_ps", tag="acc")
@@ -282,7 +288,7 @@ def tile_slstmblock_pa_kernel(
             start_weight_load(3)
 
             xn_t = early.tile([P, PACK, PASSES * B], BF16)
-            x_grouped = w_grouped.tile([P, PASSES * B, PACK], BF16, name="grouped", align_bytes=64)
+            x_grouped = early.tile([P, PASSES * B, PACK], BF16, align_bytes=64)
 
             def normed(g, t4, engine):
                 r = g * PACK + t4
@@ -300,6 +306,15 @@ def tile_slstmblock_pa_kernel(
 
             for t4 in range(PACK):
                 normed(0, t4, "s")
+
+            vec_ps = psum.tile([P, P], BF16, name="vec_ps", tag="acc")
+            nc.tensor.transpose(vec_ps[:], vec_rows[:], ident_bf16[:])
+            n_cols = len(GATES) * K_TILES
+            rb_cols = const.tile([P, n_cols], F32)
+            b_cols = const.tile([P, n_cols], F32)
+            nc.vector.tensor_copy(out=rb_cols[:], in_=vec_ps[:, n_cols : 2 * n_cols])
+            nc.vector.tensor_tensor(out=b_cols[:], in0=vec_ps[:, 0:n_cols], in1=rb_cols[:], op=ALU.add)
+
             regroup(xn_t, x_grouped, 0, nc.vector.tensor_copy)
             quantise_weight(0, (0,))
             regroup_weight(1, nc.vector.tensor_copy, (0,))
@@ -309,14 +324,6 @@ def tile_slstmblock_pa_kernel(
             regroup(xn_t, x_grouped, 1, nc.vector.tensor_copy)
             for g in range(PASSES):
                 quantise(x_grouped, x_codes, x_scales, g)
-
-            vec_ps = psum.tile([P, P], BF16, name="vec_ps", tag="acc")
-            nc.tensor.transpose(vec_ps[:], vec_rows[:], ident_bf16[:])
-            n_cols = len(GATES) * K_TILES
-            rb_cols = const.tile([P, n_cols], F32)
-            b_cols = const.tile([P, n_cols], F32)
-            nc.vector.tensor_copy(out=rb_cols[:], in_=vec_ps[:, n_cols : 2 * n_cols])
-            nc.vector.tensor_tensor(out=b_cols[:], in0=vec_ps[:, 0:n_cols], in1=rb_cols[:], op=ALU.add)
 
             regroup_weight(1, nc.scalar.copy, (1,))
             start_weight_load(4)
@@ -347,9 +354,12 @@ def tile_slstmblock_pa_kernel(
                     nc.vector.tensor_tensor(out=d[:, cols], in0=total[:], in1=big_i[:, cols], op=ALU.subtract)
                 m_new = recip[:, t, :]
                 nc.vector.scalar_tensor_tensor(out=m_new, in0=d, scalar=0.0, in1=big_i, op0=ALU.max, op1=ALU.add)
+                nc.sync.dma_start(out=rows_of(m_out, t), in_=m_new)
+
+            def exponentials(t):
+                big_i, d = pre_i[:, t, :], pre_f[:, t, :]
                 nc.scalar.activation(out=big_i, in_=d, func=ACT.Exp, scale=-1.0)
                 nc.scalar.activation(out=d, in_=d, func=ACT.Exp)
-                nc.sync.dma_start(out=rows_of(m_out, t), in_=m_new)
 
             def normaliser(t):
                 exp_minus_d, exp_d = pre_i[:, t, :], pre_f[:, t, :]
@@ -416,34 +426,41 @@ def tile_slstmblock_pa_kernel(
             input_gate(0, nc.scalar.copy)
             input_half("f", 0, ALL_S)
             input_half("f", 1, ALL_S)
-            input_gate(1, nc.scalar.copy)
             regroup_weight(4, nc.vector.tensor_copy)
             start_weight_load(7)
-            regroup_weight(5, nc.vector.tensor_copy)
+            regroup_weight(5, nc.vector.tensor_copy, (0,))
+            regroup_weight(5, nc.scalar.copy, (1,))
             quantise_weight(4)
-            quantise_weight(5)
-            regroup_weight(6, nc.scalar.copy, (0,))
+            quantise_weight(5, (0,))
+            regroup_weight(6, nc.vector.tensor_copy, (0,))
             stabiliser(0)
+            input_gate(1, nc.scalar.copy)
+            exponentials(0)
             stabiliser(1)
             input_gate(2, nc.scalar.copy)
-            regroup_weight(7, nc.vector.tensor_copy)
-            quantise_weight(7)
-            regroup_weight(6, nc.scalar.copy, (1,))
-            input_gate(3, nc.scalar.copy)
-            input_half("z", 0, ALL_S)
+            exponentials(1)
+            quantise_weight(5, (1,))
+            regroup_weight(7, nc.vector.tensor_copy, (0,))
             normaliser(0)
-            quantise_weight(6)
             stabiliser(2)
+            input_half("z", 0, ALL_S)
+            input_gate(3, nc.scalar.copy)
+            regroup_weight(7, nc.scalar.copy, (1,))
+            exponentials(2)
             input_half("z", 1, ALL_S)
             normaliser(1)
             stabiliser(3)
+            exponentials(3)
             cell_input(0)
             normaliser(2)
             cell_input(1)
+            regroup_weight(6, nc.vector.tensor_copy, (1,))
+            quantise_weight(6)
+            quantise_weight(7)
             cell_input(2)
+            normaliser(3)
             cell_input(3)
             gated_input(0)
-            normaliser(3)
             input_half("o", 0, ALL_S)
             logarithm()
             gated_input(1)

@@ -18,6 +18,7 @@ ROW_TILES = B // P
 PACK = 4
 K_PASS = P * PACK
 PASSES = DI // K_PASS
+RUN = 4
 BANK = 512
 HALVES = DH // BANK
 HEADS_PER_BANK = BANK // HD
@@ -84,9 +85,17 @@ def tile_slstmblock_pa_kernel(
             nc.sync.dma_start(out=raw[:], in_=by_pass[g])
             raw_chunk[j] = raw
 
+        def vector_regroup(out, in_):
+            nc.vector.tensor_copy(
+                out=out.rearrange("p (c i) t -> p c t i", i=RUN), in_=in_.rearrange("p t (c i) -> p c t i", i=RUN)
+            )
+
+        def scalar_regroup(out, in_):
+            nc.scalar.copy(out=out, in_=in_.rearrange("p t c -> p c t"))
+
         def regroup(rows, grouped, half, copy):
             cols = bank_columns(half)
-            copy(out=grouped[:, cols, :], in_=rows[:, :, cols].rearrange("p t c -> p c t"))
+            copy(out=grouped[:, cols, :], in_=rows[:, :, cols])
 
         def quantise(grouped, codes, scales, half):
             cols = bank_columns(half)
@@ -284,7 +293,7 @@ def tile_slstmblock_pa_kernel(
 
             transpose_h(0, nc.scalar.copy)
             transpose_h(1, nc.scalar.copy)
-            regroup_weight(0, nc.vector.tensor_copy)
+            regroup_weight(0, vector_regroup)
             start_weight_load(3)
 
             xn_t = early.tile([P, PACK, PASSES * B], BF16)
@@ -315,19 +324,19 @@ def tile_slstmblock_pa_kernel(
             nc.vector.tensor_copy(out=rb_cols[:], in_=vec_ps[:, n_cols : 2 * n_cols])
             nc.vector.tensor_tensor(out=b_cols[:], in0=vec_ps[:, 0:n_cols], in1=rb_cols[:], op=ALU.add)
 
-            regroup(xn_t, x_grouped, 0, nc.vector.tensor_copy)
+            regroup(xn_t, x_grouped, 0, vector_regroup)
             quantise_weight(0, (0,))
-            regroup_weight(1, nc.vector.tensor_copy, (0,))
+            regroup_weight(1, vector_regroup, (0,))
             for t4 in range(PACK):
                 normed(1, t4, "s" if t4 < PACK - 1 else "v")
             quantise_weight(1, (0,))
-            regroup(xn_t, x_grouped, 1, nc.vector.tensor_copy)
+            regroup(xn_t, x_grouped, 1, vector_regroup)
             for g in range(PASSES):
                 quantise(x_grouped, x_codes, x_scales, g)
 
-            regroup_weight(1, nc.scalar.copy, (1,))
+            regroup_weight(1, scalar_regroup, (1,))
             start_weight_load(4)
-            regroup_weight(2, nc.scalar.copy, (1,))
+            regroup_weight(2, scalar_regroup, (1,))
             quantise_weight(0, (1,))
             quantise_weight(1, (1,))
             transpose_h(2, nc.vector.tensor_copy)
@@ -415,9 +424,9 @@ def tile_slstmblock_pa_kernel(
             ALL_S, ALL_V = "ssss", "vvvv"
             input_half("i", 0, ALL_S)
             input_half("i", 1, ALL_S)
-            regroup_weight(2, nc.vector.tensor_copy, (0,))
+            regroup_weight(2, vector_regroup, (0,))
             start_weight_load(5)
-            regroup_weight(3, nc.vector.tensor_copy)
+            regroup_weight(3, vector_regroup)
             start_weight_load(6)
             quantise_weight(2)
             quantise_weight(3)
@@ -426,13 +435,13 @@ def tile_slstmblock_pa_kernel(
             input_gate(0, nc.scalar.copy)
             input_half("f", 0, ALL_S)
             input_half("f", 1, ALL_S)
-            regroup_weight(4, nc.vector.tensor_copy)
+            regroup_weight(4, vector_regroup)
             start_weight_load(7)
-            regroup_weight(5, nc.vector.tensor_copy, (0,))
-            regroup_weight(5, nc.scalar.copy, (1,))
+            regroup_weight(5, vector_regroup, (0,))
+            regroup_weight(5, scalar_regroup, (1,))
             quantise_weight(4)
             quantise_weight(5, (0,))
-            regroup_weight(6, nc.vector.tensor_copy, (0,))
+            regroup_weight(6, vector_regroup, (0,))
             stabiliser(0)
             input_gate(1, nc.scalar.copy)
             exponentials(0)
@@ -440,12 +449,12 @@ def tile_slstmblock_pa_kernel(
             input_gate(2, nc.scalar.copy)
             exponentials(1)
             quantise_weight(5, (1,))
-            regroup_weight(7, nc.vector.tensor_copy, (0,))
+            regroup_weight(7, vector_regroup, (0,))
             normaliser(0)
             stabiliser(2)
             input_half("z", 0, ALL_S)
             input_gate(3, nc.scalar.copy)
-            regroup_weight(7, nc.scalar.copy, (1,))
+            regroup_weight(7, scalar_regroup, (1,))
             exponentials(2)
             input_half("z", 1, ALL_S)
             normaliser(1)
@@ -454,7 +463,7 @@ def tile_slstmblock_pa_kernel(
             cell_input(0)
             normaliser(2)
             cell_input(1)
-            regroup_weight(6, nc.vector.tensor_copy, (1,))
+            regroup_weight(6, vector_regroup, (1,))
             quantise_weight(6)
             quantise_weight(7)
             cell_input(2)

@@ -208,10 +208,6 @@ def tile_slstmblock_pa_kernel(
             start_weight_load(1)
             start_weight_load(2)
             load_recurrent(state, "i")
-            load_recurrent(state, "f")
-            nc.sync.dma_start(out=m_sb[:], in_=by_row_tile(m_prev))
-            load_recurrent(state, "z")
-            load_recurrent(state, "o")
 
             minus_half = const.tile([P, 1], F32)
             nc.gpsimd.memset(minus_half[:], -0.5)
@@ -295,8 +291,10 @@ def tile_slstmblock_pa_kernel(
             transpose_h(1, nc.scalar.copy)
             regroup_weight(0, vector_regroup)
             start_weight_load(3)
+            load_recurrent(state, "f")
+            nc.sync.dma_start(out=m_sb[:], in_=by_row_tile(m_prev))
 
-            xn_t = early.tile([P, PACK, PASSES * B], BF16)
+            xn_t = [early.tile([P, PACK, B], BF16, name="xn_t%d" % g) for g in range(PASSES)]
             x_grouped = early.tile([P, PASSES * B, PACK], BF16, align_bytes=64)
 
             def normed(g, t4, engine):
@@ -304,7 +302,7 @@ def tile_slstmblock_pa_kernel(
                 y_ps = bank("y_ps")
                 for t in range(ROW_TILES):
                     nc.tensor.transpose(y_ps[:, t * P : (t + 1) * P], y[:, t, r * P : (r + 1) * P], ident_f32[:])
-                out = xn_t[:, t4, g * B : (g + 1) * B]
+                out = xn_t[g][:, t4, :]
                 gain, offset = ln_cols[:, r : r + 1], ln_cols[:, 8 + r : 9 + r]
                 if engine == "s":
                     nc.scalar.activation(out=out, in_=y_ps[:], func=ACT.Identity, bias=offset, scale=gain)
@@ -324,23 +322,25 @@ def tile_slstmblock_pa_kernel(
             nc.vector.tensor_copy(out=rb_cols[:], in_=vec_ps[:, n_cols : 2 * n_cols])
             nc.vector.tensor_tensor(out=b_cols[:], in0=vec_ps[:, 0:n_cols], in1=rb_cols[:], op=ALU.add)
 
-            regroup(xn_t, x_grouped, 0, vector_regroup)
+            vector_regroup(x_grouped[:, bank_columns(0), :], xn_t[0][:])
             quantise_weight(0, (0,))
             regroup_weight(1, vector_regroup, (0,))
             for t4 in range(PACK):
                 normed(1, t4, "s" if t4 < PACK - 1 else "v")
             quantise_weight(1, (0,))
-            regroup(xn_t, x_grouped, 1, vector_regroup)
+            vector_regroup(x_grouped[:, bank_columns(1), :], xn_t[1][:])
             for g in range(PASSES):
                 quantise(x_grouped, x_codes, x_scales, g)
 
             regroup_weight(1, scalar_regroup, (1,))
             start_weight_load(4)
+            load_recurrent(state, "z")
+            load_recurrent(state, "o")
             regroup_weight(2, scalar_regroup, (1,))
             quantise_weight(0, (1,))
             quantise_weight(1, (1,))
-            transpose_h(2, nc.vector.tensor_copy)
-            transpose_h(3, nc.vector.tensor_copy)
+            transpose_h(2, nc.scalar.copy)
+            transpose_h(3, nc.scalar.copy)
 
         with (
             tc.tile_pool(name="late", bufs=1) as late,
@@ -445,6 +445,7 @@ def tile_slstmblock_pa_kernel(
             stabiliser(0)
             input_gate(1, nc.scalar.copy)
             exponentials(0)
+            regroup_weight(6, vector_regroup, (1,))
             stabiliser(1)
             input_gate(2, nc.scalar.copy)
             exponentials(1)
@@ -458,13 +459,12 @@ def tile_slstmblock_pa_kernel(
             exponentials(2)
             input_half("z", 1, ALL_S)
             normaliser(1)
+            quantise_weight(6)
             stabiliser(3)
             exponentials(3)
             cell_input(0)
             normaliser(2)
             cell_input(1)
-            regroup_weight(6, vector_regroup, (1,))
-            quantise_weight(6)
             quantise_weight(7)
             cell_input(2)
             normaliser(3)

@@ -15,6 +15,7 @@ P = 128
 B, DI, DH, HEADS = 512, 1024, 1024, 4
 HD = DH // HEADS
 ROW_TILES = B // P
+LAST_TILE = ROW_TILES - 1
 PACK = 4
 K_PASS = P * PACK
 PASSES = DI // K_PASS
@@ -218,45 +219,48 @@ def tile_slstmblock_pa_kernel(
             ident_f32 = const.tile([P, P], F32)
             make_identity(nc, ident_f32[:])
 
-            stats = early.tile([P, 2, 2, 6], F32)
-            sums = early.tile([P, ROW_TILES, 2], F32)
-            mean_var = early.tile([P, 2, 2], F32)
-            scalar_mean = early.tile([P, ROW_TILES], F32)
+            stats = early.tile([P, LAST_TILE, 2, 6], F32)
+            sums = early.tile([P, 2], F32)
+            mean_var = early.tile([P, LAST_TILE, 2], F32)
+            scalar_mean = early.tile([P, 1], F32)
             var_eps = early.tile([P, ROW_TILES], F32)
             rstd = early.tile([P, ROW_TILES], F32)
             y = early.tile([P, ROW_TILES, DI], F32)
-
-            def vector_statistics(t):
-                for s in range(2):
-                    nc.vector.bn_stats(out=stats[:, t, s, :], in_=x_sb[:, t, s * 512 : (s + 1) * 512])
-                nc.vector.bn_aggr(out=mean_var[:, t, :], in_=stats[:, t, :, :].rearrange("p s f -> p (s f)"))
-                nc.gpsimd.tensor_scalar(
-                    out=var_eps[:, t : t + 1], in0=mean_var[:, t, 1:2], scalar1=LN_EPS, scalar2=None, op0=ALU.add
-                )
-
-            def scalar_sum(t):
-                nc.scalar.activation(out=y[:, t, :], in_=x_sb[:, t, :], func=ACT.Identity, accum_out=sums[:, t, 0:1])
-                nc.gpsimd.tensor_scalar(
-                    out=scalar_mean[:, t : t + 1], in0=sums[:, t, 0:1], scalar1=1.0 / DI, scalar2=None, op0=ALU.mult
-                )
-
-            def scalar_squares(t):
-                nc.scalar.activation(
-                    out=y[:, t, :], in_=x_sb[:, t, :], func=ACT.Square, scale=-1.0, bias=scalar_mean[:, t : t + 1],
-                    accum_out=sums[:, t, 1:2],
-                )
-                nc.gpsimd.tensor_scalar(
-                    out=var_eps[:, t : t + 1], in0=sums[:, t, 1:2], scalar1=1.0 / DI, scalar2=LN_EPS,
-                    op0=ALU.mult, op1=ALU.add,
-                )
 
             def inverse_deviation(t):
                 nc.gpsimd.tensor_tensor(
                     out=rstd[:, t : t + 1], in0=var_eps[:, t : t + 1], in1=minus_half[:], op=ALU.pow
                 )
 
+            def vector_statistics(t):
+                for s in range(2):
+                    nc.vector.bn_stats(out=stats[:, t, s, :], in_=x_sb[:, t, s * 512 : (s + 1) * 512])
+                nc.vector.bn_aggr(out=mean_var[:, t, :], in_=stats[:, t, :, :].rearrange("p s f -> p (s f)"))
+
+            def vector_variance(t):
+                nc.gpsimd.tensor_scalar(
+                    out=var_eps[:, t : t + 1], in0=mean_var[:, t, 1:2], scalar1=LN_EPS, scalar2=None, op0=ALU.add
+                )
+                inverse_deviation(t)
+
+            def scalar_sum(t):
+                nc.scalar.activation(out=y[:, t, :], in_=x_sb[:, t, :], func=ACT.Identity, accum_out=sums[:, 0:1])
+                nc.gpsimd.tensor_scalar(
+                    out=scalar_mean[:], in0=sums[:, 0:1], scalar1=1.0 / DI, scalar2=None, op0=ALU.mult
+                )
+
+            def scalar_squares(t):
+                nc.scalar.activation(
+                    out=y[:, t, :], in_=x_sb[:, t, :], func=ACT.Square, scale=-1.0, bias=scalar_mean[:],
+                    accum_out=sums[:, 1:2],
+                )
+                nc.gpsimd.tensor_scalar(
+                    out=var_eps[:, t : t + 1], in0=sums[:, 1:2], scalar1=1.0 / DI, scalar2=LN_EPS,
+                    op0=ALU.mult, op1=ALU.add,
+                )
+
             def normalise(t):
-                mean = mean_var[:, t, 0:1] if t < 2 else scalar_mean[:, t : t + 1]
+                mean = mean_var[:, t, 0:1] if t < LAST_TILE else scalar_mean[:]
                 nc.vector.tensor_scalar(
                     out=y[:, t, :].rearrange("b (g j p) -> b g j p", j=PACK, p=P),
                     in0=x_sb[:, t, :].rearrange("b (g p j) -> b g j p", j=PACK, p=P),
@@ -264,22 +268,21 @@ def tile_slstmblock_pa_kernel(
                 )
 
             vector_statistics(0)
-            inverse_deviation(0)
-            scalar_sum(2)
+            vector_variance(0)
             vector_statistics(1)
-            inverse_deviation(1)
-            scalar_sum(3)
+            scalar_sum(LAST_TILE)
             ln_cols = early.tile([P, 2 * PASSES * PACK], F32)
             nc.vector.tensor_copy(out=ln_cols[:, 0:8], in_=ln_w_raw[:].rearrange("p g t -> p (g t)"))
             nc.vector.tensor_copy(out=ln_cols[:, 8:16], in_=ln_b_raw[:].rearrange("p g t -> p (g t)"))
             normalise(0)
+            vector_variance(1)
+            scalar_squares(LAST_TILE)
+            vector_statistics(2)
             normalise(1)
-            scalar_squares(2)
-            inverse_deviation(2)
+            vector_variance(2)
             normalise(2)
-            scalar_squares(3)
-            inverse_deviation(3)
-            normalise(3)
+            inverse_deviation(LAST_TILE)
+            normalise(LAST_TILE)
 
             def transpose_h(t, copy):
                 h_ps = psum.tile([P, K_TILES, P], BF16, name="h_ps", tag="acc")
@@ -320,11 +323,10 @@ def tile_slstmblock_pa_kernel(
             rb_cols = const.tile([P, n_cols], F32)
             b_cols = const.tile([P, n_cols], F32)
             nc.vector.tensor_copy(out=rb_cols[:], in_=vec_ps[:, n_cols : 2 * n_cols])
-            nc.vector.tensor_tensor(out=b_cols[:], in0=vec_ps[:, 0:n_cols], in1=rb_cols[:], op=ALU.add)
-
-            vector_regroup(x_grouped[:, bank_columns(0), :], xn_t[0][:])
-            quantise_weight(0, (0,))
             regroup_weight(1, vector_regroup, (0,))
+            vector_regroup(x_grouped[:, bank_columns(0), :], xn_t[0][:])
+            nc.vector.tensor_tensor(out=b_cols[:], in0=vec_ps[:, 0:n_cols], in1=rb_cols[:], op=ALU.add)
+            quantise_weight(0, (0,))
             for t4 in range(PACK):
                 normed(1, t4, "s" if t4 < PACK - 1 else "v")
             quantise_weight(1, (0,))
@@ -358,11 +360,11 @@ def tile_slstmblock_pa_kernel(
 
             def stabiliser(t):
                 big_i, d = pre_i[:, t, :], pre_f[:, t, :]
+                m_new = recip[:, t, :]
                 for half, total in enumerate(sum_banks("f", t)):
                     cols = bank_columns(half)
                     nc.vector.tensor_tensor(out=d[:, cols], in0=total[:], in1=big_i[:, cols], op=ALU.subtract)
-                m_new = recip[:, t, :]
-                nc.vector.scalar_tensor_tensor(out=m_new, in0=d, scalar=0.0, in1=big_i, op0=ALU.max, op1=ALU.add)
+                    nc.vector.tensor_tensor(out=m_new[:, cols], in0=total[:], in1=big_i[:, cols], op=ALU.max)
                 nc.sync.dma_start(out=rows_of(m_out, t), in_=m_new)
 
             def exponentials(t):

import math

import concourse.mybir as mybir
from concourse.masks import make_identity

F32 = mybir.dt.float32
BF16 = mybir.dt.bfloat16
U32 = mybir.dt.uint32
U8 = mybir.dt.uint8
FP8X4 = mybir.dt.float8_e4m3fn_x4
ALU = mybir.AluOpType
ACT = mybir.ActivationFunctionType

P = 128
B, DI, DH, HEADS = 512, 1024, 1024, 4
HD = DH // HEADS
ROW_TILES = B // P
LAST_TILE = ROW_TILES - 1
PACK = 4
K_PASS = P * PACK
PASSES = DI // K_PASS
RUN = 4
BANK = 512
HALVES = DH // BANK
HEADS_PER_BANK = BANK // HD
K_TILES = DH // P
K_TILES_PER_HEAD = HD // P
LN_EPS = 1e-5
N_EPS = 1e-13
GATES = ("i", "f", "z", "o")
RAW_AHEAD = 3

FLOPS = 2 * B * DI * DH * 4 + 2 * B * DH * HD * 4


def bank_columns(half):
    return slice(half * BANK, (half + 1) * BANK)


def tile_slstmblock_pa_kernel(
    tc, x, h_prev, c_prev, n_prev, m_prev, ln_w, ln_b,
    Wz, b_z, Rz, rb_z, Wi, b_i, Ri, rb_i, Wf, b_f, Rf, rb_f, Wo, b_o, Ro, rb_o,
    out_0, out_1, out_2, out_3,
):
    nc = tc.nc
    weight = {"z": Wz, "i": Wi, "f": Wf, "o": Wo}
    recurrent = {"z": Rz, "i": Ri, "f": Rf, "o": Ro}
    biases = {"z": (b_z, rb_z), "i": (b_i, rb_i), "f": (b_f, rb_f), "o": (b_o, rb_o)}
    h_out, c_out, n_out, m_out = out_0, out_1, out_2, out_3

    def rows_of(dram, t):
        return dram[t * P : (t + 1) * P, :]

    def by_row_tile(dram):
        return dram.rearrange("(t p) n -> p t n", p=P)

    with (
        tc.manual_schedule(),
        tc.tile_pool(name="const", bufs=1) as const,
        tc.tile_pool(name="state", bufs=1) as state,
        tc.tile_pool(name="w_raw", bufs=RAW_AHEAD) as w_raw,
        tc.tile_pool(name="w_grouped", bufs=3) as w_grouped,
        tc.tile_pool(name="w_quant", bufs=2 * PASSES) as w_quant,
        tc.tile_pool(name="in_t", bufs=2 * HALVES) as in_pool,
        tc.psum_pool(name="psum", bufs=4) as psum,
    ):
        pre_i = state.tile([P, ROW_TILES, DH], F32)
        pre_f = state.tile([P, ROW_TILES, DH], F32)
        x_codes = state.tile([P, PASSES * B], U32, align_bytes=64)
        x_scales = state.tile([P, PASSES * B], U8, align_bytes=64)
        h_t = state.tile([P, K_TILES, B], BF16)
        m_sb = state.tile([P, ROW_TILES, DH], BF16)
        r_sb = {}

        chunks = [(gate, g) for gate in GATES for g in range(PASSES)]
        raw_chunk = {}
        grouped_chunk = {}
        in_halves = {}
        w_codes = {}
        w_scales = {}

        def start_weight_load(j):
            gate, g = chunks[j]
            raw = w_raw.tile([P, PACK, DH], BF16, name="raw")
            by_pass = weight[gate].rearrange("(g p t) n -> g p t n", t=PACK, p=P)
            nc.sync.dma_start(out=raw[:], in_=by_pass[g])
            raw_chunk[j] = raw

        def vector_regroup(out, in_):
            nc.vector.tensor_copy(
                out=out.rearrange("p (c i) t -> p c t i", i=RUN), in_=in_.rearrange("p t (c i) -> p c t i", i=RUN)
            )

        def scalar_regroup(out, in_):
            nc.scalar.copy(out=out, in_=in_.rearrange("p t c -> p c t"))

        def regroup(rows, grouped, half, copy):
            cols = bank_columns(half)
            copy(out=grouped[:, cols, :], in_=rows[:, :, cols])

        def quantise(grouped, codes, scales, half):
            cols = bank_columns(half)
            nc.vector.quantize_mx(
                out=codes[:, cols].bitcast(FP8X4),
                scales=scales[:, cols],
                in_=grouped[:, cols, :].rearrange("p c t -> p (c t)"),
            )

        def regroup_weight(j, copy, halves=(0, 1)):
            if j not in grouped_chunk:
                grouped_chunk[j] = w_grouped.tile([P, DH, PACK], BF16, name="grouped", align_bytes=64)
            for half in halves:
                regroup(raw_chunk[j], grouped_chunk[j], half, copy)

        def quantise_weight(j, halves=(0, 1)):
            key = chunks[j]
            if key not in w_codes:
                w_codes[key] = w_quant.tile([P, DH], U32, name="codes", align_bytes=64)
                w_scales[key] = w_quant.tile([P, DH], U8, name="scales", align_bytes=64)
            for half in halves:
                quantise(grouped_chunk[j], w_codes[key], w_scales[key], half)

        def load_recurrent(pool, gate):
            r_sb[gate] = pool.tile([P, K_TILES, HD], BF16, name="r_" + gate)
            nc.sync.dma_start(
                out=r_sb[gate][:], in_=recurrent[gate].rearrange("h (kt p) n -> p (h kt) n", p=P)
            )

        def bank(name, tag="acc"):
            return psum.tile([P, BANK], F32, name=name, tag=tag)

        def input_half(gate, half, copies):
            in_t = in_pool.tile([P, BANK // P, B], F32, name="in_t")
            for q, engine in enumerate(copies):
                block = half * (BANK // P) + q
                cols = slice(block * P, (block + 1) * P)
                acc = bank("acc")
                for g in range(PASSES):
                    rows = slice(g * B, (g + 1) * B)
                    nc.tensor.matmul_mx(
                        out=acc[:],
                        lhsT=w_codes[(gate, g)][:, cols].bitcast(FP8X4),
                        lhsT_scale=w_scales[(gate, g)][:, cols],
                        rhs=x_codes[:, rows].bitcast(FP8X4),
                        rhs_scale=x_scales[:, rows],
                        start=(g == 0),
                        stop=(g == PASSES - 1),
                    )
                c = GATES.index(gate) * K_TILES + block
                bias = b_cols[:, c : c + 1]
                if engine == "s":
                    nc.scalar.activation(out=in_t[:, q, :], in_=acc[:], func=ACT.Identity, bias=bias)
                else:
                    nc.vector.tensor_scalar(out=in_t[:, q, :], in0=acc[:], scalar1=bias, scalar2=None, op0=ALU.add)
            in_halves[(gate, half)] = in_t

        def sum_bank(gate, t, half):
            total = bank("total", tag="total")
            for q in range(BANK // P):
                nc.tensor.matmul(
                    out=total[:, q * P : (q + 1) * P],
                    lhsT=in_halves[(gate, half)][:, q, t * P : (t + 1) * P],
                    rhs=ident_f32[:], is_transpose=True, start=(q == 0), stop=False,
                )
            if gate == "f":
                nc.tensor.matmul(
                    out=total[:], lhsT=ident_bf16[:], rhs=m_sb[:, t, bank_columns(half)], start=False, stop=False
                )
            for hh in range(HEADS_PER_BANK):
                head = half * HEADS_PER_BANK + hh
                for kt in range(K_TILES_PER_HEAD):
                    k_tile = head * K_TILES_PER_HEAD + kt
                    nc.tensor.matmul(
                        out=total[:, hh * HD : (hh + 1) * HD],
                        lhsT=h_t[:, k_tile, t * P : (t + 1) * P],
                        rhs=r_sb[gate][:, k_tile, :],
                        start=False,
                        stop=(hh == HEADS_PER_BANK - 1 and kt == K_TILES_PER_HEAD - 1),
                    )
            return total

        def sum_banks(gate, t):
            return (sum_bank(gate, t, half) for half in range(HALVES))

        with tc.tile_pool(name="early", bufs=1) as early:
            x_sb = early.tile([P, ROW_TILES, DI], BF16)
            for t in range(ROW_TILES):
                nc.sync.dma_start(out=x_sb[:, t, :], in_=rows_of(x, t))
            ln_w_raw = early.tile([P, PASSES, PACK], BF16)
            ln_b_raw = early.tile([P, PASSES, PACK], BF16)
            nc.scalar.dma_start(out=ln_w_raw[:], in_=ln_w.rearrange("(g p t) -> p g t", p=P, t=PACK))
            nc.scalar.dma_start(out=ln_b_raw[:], in_=ln_b.rearrange("(g p t) -> p g t", p=P, t=PACK))
            h_sb = early.tile([P, ROW_TILES, DH], BF16)
            nc.sync.dma_start(out=h_sb[:], in_=by_row_tile(h_prev))
            vec_rows = early.tile([P, P], BF16)
            nc.vector.memset(vec_rows[:], 0.0)
            vecs = [biases[gate][k] for k in range(2) for gate in GATES]

            def load_bias(v):
                nc.sync.dma_start(
                    out=vec_rows[v * K_TILES : (v + 1) * K_TILES, :], in_=vecs[v].rearrange("(r c) -> r c", c=P)
                )

            for v in range(4):
                load_bias(v)
            start_weight_load(0)
            for v in range(4, 8):
                load_bias(v)
            start_weight_load(1)
            start_weight_load(2)
            load_recurrent(state, "i")

            minus_half = const.tile([P, 1], F32)
            nc.gpsimd.memset(minus_half[:], -0.5)
            warm = const.tile([P, 1], F32)
            nc.scalar.activation(out=warm[:], in_=minus_half[:], func=ACT.Exp)
            ident_bf16 = const.tile([P, P], BF16)
            make_identity(nc, ident_bf16[:])
            ident_f32 = const.tile([P, P], F32)
            make_identity(nc, ident_f32[:])

            stats = early.tile([P, LAST_TILE, 2, 6], F32)
            sums = early.tile([P, 2], F32)
            mean_var = early.tile([P, LAST_TILE, 2], F32)
            scalar_mean = early.tile([P, 1], F32)
            var_eps = early.tile([P, ROW_TILES], F32)
            rstd = early.tile([P, ROW_TILES], F32)
            y = early.tile([P, ROW_TILES, DI], F32)

            def inverse_deviation(t):
                nc.gpsimd.tensor_tensor(
                    out=rstd[:, t : t + 1], in0=var_eps[:, t : t + 1], in1=minus_half[:], op=ALU.pow
                )

            def vector_statistics(t):
                for s in range(2):
                    nc.vector.bn_stats(out=stats[:, t, s, :], in_=x_sb[:, t, s * 512 : (s + 1) * 512])
                nc.vector.bn_aggr(out=mean_var[:, t, :], in_=stats[:, t, :, :].rearrange("p s f -> p (s f)"))

            def vector_variance(t):
                nc.gpsimd.tensor_scalar(
                    out=var_eps[:, t : t + 1], in0=mean_var[:, t, 1:2], scalar1=LN_EPS, scalar2=None, op0=ALU.add
                )
                inverse_deviation(t)

            def scalar_sum(t):
                nc.scalar.activation(out=y[:, t, :], in_=x_sb[:, t, :], func=ACT.Identity, accum_out=sums[:, 0:1])
                nc.gpsimd.tensor_scalar(
                    out=scalar_mean[:], in0=sums[:, 0:1], scalar1=1.0 / DI, scalar2=None, op0=ALU.mult
                )

            def scalar_squares(t):
                nc.scalar.activation(
                    out=y[:, t, :], in_=x_sb[:, t, :], func=ACT.Square, scale=-1.0, bias=scalar_mean[:],
                    accum_out=sums[:, 1:2],
                )
                nc.gpsimd.tensor_scalar(
                    out=var_eps[:, t : t + 1], in0=sums[:, 1:2], scalar1=1.0 / DI, scalar2=LN_EPS,
                    op0=ALU.mult, op1=ALU.add,
                )

            def normalise(t):
                mean = mean_var[:, t, 0:1] if t < LAST_TILE else scalar_mean[:]
                nc.vector.tensor_scalar(
                    out=y[:, t, :].rearrange("b (g j p) -> b g j p", j=PACK, p=P),
                    in0=x_sb[:, t, :].rearrange("b (g p j) -> b g j p", j=PACK, p=P),
                    scalar1=mean, scalar2=rstd[:, t : t + 1], op0=ALU.subtract, op1=ALU.mult,
                )

            vector_statistics(0)
            vector_variance(0)
            vector_statistics(1)
            scalar_sum(LAST_TILE)
            ln_cols = early.tile([P, 2 * PASSES * PACK], F32)
            nc.vector.tensor_copy(out=ln_cols[:, 0:8], in_=ln_w_raw[:].rearrange("p g t -> p (g t)"))
            nc.vector.tensor_copy(out=ln_cols[:, 8:16], in_=ln_b_raw[:].rearrange("p g t -> p (g t)"))
            normalise(0)
            vector_variance(1)
            scalar_squares(LAST_TILE)
            vector_statistics(2)
            normalise(1)
            vector_variance(2)
            normalise(2)
            inverse_deviation(LAST_TILE)
            normalise(LAST_TILE)

            def transpose_h(t, copy):
                h_ps = psum.tile([P, K_TILES, P], BF16, name="h_ps", tag="acc")
                for kt in range(K_TILES):
                    nc.tensor.transpose(h_ps[:, kt, :], h_sb[:, t, kt * P : (kt + 1) * P], ident_bf16[:])
                copy(out=h_t[:, :, t * P : (t + 1) * P], in_=h_ps[:])

            transpose_h(0, nc.scalar.copy)
            transpose_h(1, nc.scalar.copy)
            regroup_weight(0, vector_regroup)
            start_weight_load(3)
            load_recurrent(state, "f")
            nc.sync.dma_start(out=m_sb[:], in_=by_row_tile(m_prev))

            xn_t = [early.tile([P, PACK, B], BF16, name="xn_t%d" % g) for g in range(PASSES)]
            x_grouped = early.tile([P, PASSES * B, PACK], BF16, align_bytes=64)

            def normed(g, t4, engine):
                r = g * PACK + t4
                y_ps = bank("y_ps")
                for t in range(ROW_TILES):
                    nc.tensor.transpose(y_ps[:, t * P : (t + 1) * P], y[:, t, r * P : (r + 1) * P], ident_f32[:])
                out = xn_t[g][:, t4, :]
                gain, offset = ln_cols[:, r : r + 1], ln_cols[:, 8 + r : 9 + r]
                if engine == "s":
                    nc.scalar.activation(out=out, in_=y_ps[:], func=ACT.Identity, bias=offset, scale=gain)
                else:
                    nc.vector.tensor_scalar(
                        out=out, in0=y_ps[:], scalar1=gain, scalar2=offset, op0=ALU.mult, op1=ALU.add
                    )

            for t4 in range(PACK):
                normed(0, t4, "s")

            vec_ps = psum.tile([P, P], BF16, name="vec_ps", tag="acc")
            nc.tensor.transpose(vec_ps[:], vec_rows[:], ident_bf16[:])
            n_cols = len(GATES) * K_TILES
            rb_cols = const.tile([P, n_cols], F32)
            b_cols = const.tile([P, n_cols], F32)
            nc.vector.tensor_copy(out=rb_cols[:], in_=vec_ps[:, n_cols : 2 * n_cols])
            regroup_weight(1, vector_regroup, (0,))
            vector_regroup(x_grouped[:, bank_columns(0), :], xn_t[0][:])
            nc.vector.tensor_tensor(out=b_cols[:], in0=vec_ps[:, 0:n_cols], in1=rb_cols[:], op=ALU.add)
            quantise_weight(0, (0,))
            for t4 in range(PACK):
                normed(1, t4, "s" if t4 < PACK - 1 else "v")
            quantise_weight(1, (0,))
            vector_regroup(x_grouped[:, bank_columns(1), :], xn_t[1][:])
            for g in range(PASSES):
                quantise(x_grouped, x_codes, x_scales, g)

            regroup_weight(1, scalar_regroup, (1,))
            start_weight_load(4)
            load_recurrent(state, "z")
            load_recurrent(state, "o")
            regroup_weight(2, scalar_regroup, (1,))
            quantise_weight(0, (1,))
            quantise_weight(1, (1,))
            transpose_h(2, nc.scalar.copy)
            transpose_h(3, nc.scalar.copy)

        with (
            tc.tile_pool(name="late", bufs=1) as late,
            tc.tile_pool(name="stream", bufs=ROW_TILES) as stream,
        ):
            n_sb = late.tile([P, ROW_TILES, DH], BF16)
            c_sb = late.tile([P, ROW_TILES, DH], BF16)
            n_new = late.tile([P, ROW_TILES, DH], F32)
            recip = late.tile([P, ROW_TILES, DH], F32)
            z = {}

            def input_gate(t, copy):
                for half, total in enumerate(sum_banks("i", t)):
                    copy(out=pre_i[:, t, bank_columns(half)], in_=total[:])

            def stabiliser(t):
                big_i, d = pre_i[:, t, :], pre_f[:, t, :]
                m_new = recip[:, t, :]
                for half, total in enumerate(sum_banks("f", t)):
                    cols = bank_columns(half)
                    nc.vector.tensor_tensor(out=d[:, cols], in0=total[:], in1=big_i[:, cols], op=ALU.subtract)
                    nc.vector.tensor_tensor(out=m_new[:, cols], in0=total[:], in1=big_i[:, cols], op=ALU.max)
                nc.sync.dma_start(out=rows_of(m_out, t), in_=m_new)

            def exponentials(t):
                big_i, d = pre_i[:, t, :], pre_f[:, t, :]
                nc.scalar.activation(out=big_i, in_=d, func=ACT.Exp, scale=-1.0)
                nc.scalar.activation(out=d, in_=d, func=ACT.Exp)

            def normaliser(t):
                exp_minus_d, exp_d = pre_i[:, t, :], pre_f[:, t, :]
                nc.vector.scalar_tensor_tensor(
                    out=n_new[:, t, :], in0=exp_d, scalar=1.0, in1=n_sb[:, t, :], op0=ALU.min, op1=ALU.mult
                )
                nc.vector.scalar_tensor_tensor(
                    out=exp_d, in0=exp_d, scalar=1.0, in1=c_sb[:, t, :], op0=ALU.min, op1=ALU.mult
                )
                nc.vector.scalar_tensor_tensor(
                    out=n_new[:, t, :], in0=exp_minus_d, scalar=1.0, in1=n_new[:, t, :], op0=ALU.min, op1=ALU.add
                )
                nc.sync.dma_start(out=rows_of(n_out, t), in_=n_new[:, t, :])

            def tanh_gate(gate, t, out, scale):
                for half, total in enumerate(sum_banks(gate, t)):
                    nc.scalar.activation(out=out[:, bank_columns(half)], in_=total[:], func=ACT.Tanh, scale=scale)

            def cell_input(t):
                z[t] = stream.tile([P, DH], F32, name="z")
                tanh_gate("z", t, z[t], 1.0)

            def output_gate(t):
                tanh_gate("o", t, pre_i[:, t, :], 0.5)

            def logarithm():
                nc.scalar.activation(out=recip[:], in_=n_new[:], func=ACT.Ln, bias=N_EPS)

            def reciprocal(t):
                nc.scalar.activation(
                    out=recip[:, t, :], in_=recip[:, t, :], func=ACT.Exp, bias=math.log(0.5), scale=-1.0
                )

            def gated_input(t):
                nc.vector.scalar_tensor_tensor(
                    out=z[t][:], in0=pre_i[:, t, :], scalar=1.0, in1=z[t][:], op0=ALU.min, op1=ALU.mult
                )

            def new_cell(t):
                f_c = pre_f[:, t, :]
                nc.vector.tensor_tensor(out=f_c, in0=f_c, in1=z[t][:], op=ALU.add)
                nc.sync.dma_start(out=rows_of(c_out, t), in_=f_c)

            def cell_over_n(t):
                nc.vector.tensor_tensor(out=recip[:, t, :], in0=recip[:, t, :], in1=pre_f[:, t, :], op=ALU.mult)

            def new_hidden(t):
                nc.vector.scalar_tensor_tensor(
                    out=recip[:, t, :], in0=pre_i[:, t, :], scalar=1.0, in1=recip[:, t, :], op0=ALU.add, op1=ALU.mult
                )
                nc.sync.dma_start(out=rows_of(h_out, t), in_=recip[:, t, :])

            ALL_S, ALL_V = "ssss", "vvvv"
            input_half("i", 0, ALL_S)
            input_half("i", 1, ALL_S)
            regroup_weight(2, vector_regroup, (0,))
            start_weight_load(5)
            regroup_weight(3, vector_regroup)
            start_weight_load(6)
            quantise_weight(2)
            quantise_weight(3)
            nc.sync.dma_start(out=n_sb[:], in_=by_row_tile(n_prev))
            nc.sync.dma_start(out=c_sb[:], in_=by_row_tile(c_prev))
            input_gate(0, nc.scalar.copy)
            input_half("f", 0, ALL_S)
            input_half("f", 1, ALL_S)
            regroup_weight(4, vector_regroup)
            start_weight_load(7)
            regroup_weight(5, vector_regroup, (0,))
            regroup_weight(5, scalar_regroup, (1,))
            quantise_weight(4)
            quantise_weight(5, (0,))
            regroup_weight(6, vector_regroup, (0,))
            stabiliser(0)
            input_gate(1, nc.scalar.copy)
            exponentials(0)
            regroup_weight(6, vector_regroup, (1,))
            stabiliser(1)
            input_gate(2, nc.scalar.copy)
            exponentials(1)
            quantise_weight(5, (1,))
            regroup_weight(7, vector_regroup, (0,))
            normaliser(0)
            stabiliser(2)
            input_half("z", 0, ALL_S)
            input_gate(3, nc.scalar.copy)
            regroup_weight(7, scalar_regroup, (1,))
            exponentials(2)
            input_half("z", 1, ALL_S)
            normaliser(1)
            quantise_weight(6)
            stabiliser(3)
            exponentials(3)
            cell_input(0)
            normaliser(2)
            cell_input(1)
            quantise_weight(7)
            cell_input(2)
            normaliser(3)
            cell_input(3)
            gated_input(0)
            input_half("o", 0, ALL_S)
            logarithm()
            gated_input(1)
            new_cell(0)
            new_cell(1)
            input_half("o", 1, ALL_V)
            gated_input(2)
            gated_input(3)
            reciprocal(0)
            output_gate(0)
            new_cell(2)
            reciprocal(1)
            new_cell(3)
            output_gate(1)
            cell_over_n(0)
            reciprocal(2)
            output_gate(2)
            new_hidden(0)
            cell_over_n(1)
            reciprocal(3)
            output_gate(3)
            new_hidden(1)
            cell_over_n(2)
            cell_over_n(3)
            new_hidden(2)
            new_hidden(3)
